import numpy as np
import ml_dtypes

BF16 = ml_dtypes.bfloat16


def bf(x):
    return np.asarray(x, np.float32).astype(BF16)


def f32(x):
    return np.asarray(x, np.float32)


def f64(x):
    return np.asarray(x).astype(np.float64)


def striped(idx):
    return np.tile(idx.reshape(-1, 16).T, (8, 1))


V, D, HALF, M, H, HK, REP, SINK, N = 4096, 128, 64, 256, 4, 2, 2, 128, 1536
BASE = 10000.0
SCALE = 0.08838834764831845
VSCALE = 3.0


def rope_cache():
    inv_freq = 1.0 / BASE ** (np.arange(HALF) / HALF)
    th = np.outer(np.arange(V), inv_freq)
    return np.concatenate([np.cos(th), np.sin(th)], axis=1)


def spread_matrix():
    w = np.zeros((D, M))
    i = np.arange(HALF)
    w[i, i] = 1.0
    w[i, HALF + i] = 1.0
    w[HALF + i, D + i] = -1.0
    w[HALF + i, D + HALF + i] = 1.0
    return w


def setup_inputs():
    return {"table": bf(rope_cache()), "spread": bf(spread_matrix()), "q": f32(np.random.standard_normal((H * D, N))), "k": f32(np.random.standard_normal((HK * D, N))), "v": bf(VSCALE * np.random.standard_normal((N, HK * D))), "sink_k": bf(np.random.standard_normal((HK * D, SINK))), "sink_v": bf(VSCALE * np.random.standard_normal((SINK, HK * D))), "offs": striped(np.random.permutation(V)[:N])}


def rope(x, heads, cosf, sinf):
    x = x.reshape(heads, D, N)
    xs = np.concatenate([x[:, HALF:], x[:, :HALF]], axis=1)
    return x * cosf[None] + xs * sinf[None]


def reference(table, spread, q, k, v, sink_k, sink_v, offs):
    idx = offs[:16].T.reshape(-1)
    cs = f64(spread).T @ f64(table)[idx].T
    cosf, sinf = cs[:D], cs[D:]
    qr = rope(f64(q), H, cosf, sinf)
    kr = rope(f64(k), HK, cosf, sinf)
    kf = np.concatenate([f64(sink_k).reshape(HK, D, SINK), kr], axis=2)
    vf = np.concatenate([f64(sink_v), f64(v)], axis=0).reshape(SINK + N, HK, D)
    vis = np.arange(SINK + N)[:, None] <= np.arange(N)[None, :] + SINK
    res = np.zeros((H, D, N))
    for h in range(H):
        a = h // REP
        sc = SCALE * (kf[a].T @ qr[h])
        e = np.where(vis, np.exp(sc), 0.0)
        res[h] = (vf[:, a].T @ e) / e.sum(axis=0, keepdims=True)
    return res.reshape(H * D, N)

@@ -1,0 +1,182 @@
+import concourse.mybir as mybir
+from concourse.masks import make_identity
+
+BF16, F32, I32, U16 = mybir.dt.bfloat16, mybir.dt.float32, mybir.dt.int32, mybir.dt.uint16
+MULT, ADD, MIN, IS_GE = mybir.AluOpType.mult, mybir.AluOpType.add, mybir.AluOpType.min, mybir.AluOpType.is_ge
+EXP = mybir.ActivationFunctionType.Exp
+
+P = 128
+HALF = 64
+POSITIONS = 4096
+N = 1536
+H, HK = 4, 2
+PAIR = H // HK
+SCALE = 0.08838834764831845
+BLOCKS = N // P
+PIECE = 512
+BLOCKS_IN_PIECE = PIECE // P
+V_STEP = 144
+HUGE = 3.0e38
+LEAD = 1
+SUM_LAG = 3
+TURN_LAG = 2
+
+VISIBLE = P * N + N * (N + 1) // 2
+FLOPS = 2 * P * 2 * P * N + H * VISIBLE * 2 * P * 2
+
+
+def tile_openpangusinkattention_b_kernel(tc, table, spread, q, k, v, sink_k, sink_v, offs, out):
+    nc = tc.nc
+    q_rows = q.rearrange("(h d) n -> d h n", d=P)
+    k_rows = k.rearrange("(a d) n -> d a n", d=P)
+    q_halves = q.rearrange("(h s d) n -> s d h n", s=2, d=HALF)
+    k_halves = k.rearrange("(a s d) n -> s d a n", s=2, d=HALF)
+    v_blocks = v.rearrange("(b t) (a d) -> b t a d", t=P, a=HK)
+    out_rows = out.rearrange("(h d) n -> d h n", d=P)
+
+    with (
+        tc.tile_pool(name="held", bufs=1) as held,
+        tc.tile_pool(name="raw", bufs=BLOCKS) as raw,
+        tc.tile_pool(name="exps", bufs=SUM_LAG + 2) as exps,
+        tc.tile_pool(name="results", bufs=3) as results,
+        tc.psum_pool(name="cs_banks", bufs=1) as cs_banks,
+        tc.psum_pool(name="score_banks", bufs=3) as score_banks,
+        tc.psum_pool(name="sum_banks", bufs=2) as sum_banks,
+        tc.psum_pool(name="turn_banks", bufs=1) as turn_banks,
+    ):
+        offsets = held.tile([P, N // 16], U16, name="offsets")
+        nc.sync.dma_start(offsets[:], offs)
+
+        table_rows = held.tile([P, POSITIONS // P, P], BF16, name="table_rows")
+        table_blocks = table.rearrange("(b p) f -> p b f", p=P)
+        for g in range(4):
+            queue = nc.sync if g % 2 == 0 else nc.scalar
+            queue.dma_start(table_rows[:, 8 * g : 8 * g + 8, :], table_blocks[:, 8 * g : 8 * g + 8, :])
+        spread_sb = held.tile([P, 2 * P], BF16, name="spread_sb")
+        nc.scalar.dma_start(spread_sb[:], spread)
+
+        v_ones = held.tile([P, BLOCKS + 1, HK, V_STEP], BF16, name="v_ones")
+        nc.gpsimd.memset(v_ones[:, :, :, P:V_STEP], 1.0)
+        sink_keys = held.tile([P, HK, P], BF16, name="sink_keys")
+
+        x_of, x_swap_of = [], []
+        for b in range(BLOCKS):
+            cols = slice(b * P, (b + 1) * P)
+            x = raw.tile([P, H + HK, P], F32, name="x")
+            x_swap = raw.tile([P, H + HK, P], F32, name="x_swap")
+            nc.sync.dma_start(x[:, 0:H, :], q_rows[:, :, cols])
+            nc.sync.dma_start(x[:, H:, :], k_rows[:, :, cols])
+            for s in range(2):
+                rows = slice(s * HALF, (s + 1) * HALF)
+                nc.sync.dma_start(x_swap[rows, 0:H, :], q_halves[1 - s, :, :, cols])
+                nc.sync.dma_start(x_swap[rows, H:, :], k_halves[1 - s, :, :, cols])
+            nc.sync.dma_start(v_ones[:, b + 1, :, 0:P], v_blocks[b, :, :, :])
+            x_of.append(x)
+            x_swap_of.append(x_swap)
+            if b == 0:
+                nc.sync.dma_start(sink_keys[:], sink_k.rearrange("(a d) t -> d a t", d=P))
+                nc.sync.dma_start(v_ones[:, 0, :, 0:P], sink_v.rearrange("t (a d) -> t a d", a=HK))
+
+        identity_bf16 = held.tile([P, P], BF16, name="identity_bf16")
+        make_identity(nc, identity_bf16[:])
+        identity_f32 = held.tile([P, P], F32, name="identity_f32")
+        make_identity(nc, identity_f32[:])
+        warm = held.tile([P, 1], F32, name="warm")
+        nc.vector.memset(warm[:], 0.0)
+        nc.scalar.activation(warm[:], warm[:], EXP)
+
+        window = held.tile([P, POSITIONS], BF16, name="window")
+        for g in range(4):
+            turned_rows = score_banks.tile([P, 8 * P], BF16, name="turned_rows", tag="scores")
+            for b in range(8):
+                nc.tensor.transpose(turned_rows[:, b * P : (b + 1) * P], table_rows[:, 8 * g + b, :], identity_bf16[:])
+            if g % 2 == 0:
+                nc.vector.tensor_copy(window[:, g * 8 * P : (g + 1) * 8 * P], turned_rows[:])
+            else:
+                nc.scalar.copy(window[:, g * 8 * P : (g + 1) * 8 * P], turned_rows[:])
+
+        rotated = held.tile([P, BLOCKS, H + HK, P], BF16, name="rotated")
+
+        distance = held.tile([P, PAIR, P], I32, name="distance")
+        nc.gpsimd.iota(distance[:], pattern=[[0, PAIR], [1, P]], base=0, channel_multiplier=-1)
+        cap = held.tile([P, PAIR, P], BF16, name="cap")
+        nc.vector.tensor_scalar(cap[:], distance[:], 0.0, HUGE, IS_GE, MULT)
+
+        cs_of, e_of, sums_of, by_query_of = {}, {}, {}, {}
+
+        def look_up(piece):
+            piece_offsets = offsets[:, piece * (PIECE // 16) : (piece + 1) * (PIECE // 16)]
+            cs = cs_banks.tile([P, 2, PIECE], F32, name="cs")
+            for half in range(2):
+                nc.tensor.matmul(
+                    cs[:, half, :], spread_sb[:, half * P : (half + 1) * P], window[:].indirect(piece_offsets),
+                    start=True, stop=True,
+                )
+            return cs
+
+        def rotate(b):
+            piece = b // BLOCKS_IN_PIECE
+            if b % BLOCKS_IN_PIECE == 0:
+                cs_of[piece] = look_up(piece)
+            cs = cs_of[piece]
+            cols = slice((b % BLOCKS_IN_PIECE) * P, (b % BLOCKS_IN_PIECE + 1) * P)
+            x, x_swap = x_of[b], x_swap_of[b]
+            all_heads = [P, H + HK, P]
+            nc.vector.tensor_tensor(x[:], x[:], cs[:, 0, cols].unsqueeze(1).to_broadcast(all_heads), MULT)
+            nc.vector.tensor_tensor(x_swap[:], x_swap[:], cs[:, 1, cols].unsqueeze(1).to_broadcast(all_heads), MULT)
+            nc.gpsimd.tensor_tensor(rotated[:, b, :, :], x[:], x_swap[:], ADD)
+
+        def weigh(b, a, first):
+            key_blocks = range(first, min(first + 2, b + 2))
+            scores = score_banks.tile([P, 2, PAIR, P], F32, name="scores", tag="scores")
+            for i, t in enumerate(key_blocks):
+                keys = sink_keys[:, a, :] if t == 0 else rotated[:, t - 1, H + a, :]
+                nc.tensor.matmul(scores[:, i, :, :], keys, rotated[:, b, PAIR * a : PAIR * (a + 1), :], start=True, stop=True)
+            e = exps.tile([P, 2, PAIR, P], BF16, name="e")
+            count = len(key_blocks)
+            nc.scalar.activation(e[:, 0:count, :, :], scores[:, 0:count, :, :], EXP, scale=SCALE)
+            if key_blocks[-1] == b + 1:
+                nc.vector.tensor_tensor(e[:, count - 1, :, :], e[:, count - 1, :, :], cap[:], MIN)
+            return e
+
+        def add_up(b, a, first, e):
+            if first == 0:
+                sums_of[a] = sum_banks.tile([P, PAIR, P + 1], F32, name="sums")
+            sums = sums_of[a]
+            for i, t in enumerate(range(first, min(first + 2, b + 2))):
+                for h in range(PAIR):
+                    nc.tensor.matmul(
+                        sums[:, h, :], e[:, i, h, :], v_ones[:, t, a, 0 : P + 1],
+                        start=(t == 0 and h == 0), stop=(t == b + 1 and h == PAIR - 1),
+                    )
+            if first + 2 >= b + 2:
+                reciprocal = results.tile([P, PAIR, 1], F32, name="reciprocal")
+                nc.vector.reciprocal(reciprocal[:], sums[:, :, P : P + 1])
+                by_query = results.tile([P, PAIR, P], F32, name="by_query")
+                nc.vector.tensor_tensor(by_query[:], sums[:, :, 0:P], reciprocal[:].to_broadcast([P, PAIR, P]), MULT)
+                by_query_of[a] = by_query
+
+        def finish(b, a):
+            turned = turn_banks.tile([P, PAIR, P], F32, name="turned")
+            for h in range(PAIR):
+                nc.tensor.transpose(turned[:, h, :], by_query_of[a][:, h, :], identity_f32[:])
+            by_feature = results.tile([P, PAIR, P], F32, name="by_feature")
+            nc.vector.tensor_copy(by_feature[:], turned[:])
+            nc.sync.dma_start(out_rows[:, PAIR * a : PAIR * (a + 1), b * P : (b + 1) * P], by_feature[:])
+
+        steps = [(b, a, first) for b in range(BLOCKS) for a in range(HK) for first in range(0, b + 2, 2)]
+        for b in range(LEAD):
+            rotate(b)
+        for s in range(len(steps) + SUM_LAG + TURN_LAG):
+            if s < len(steps):
+                b, a, first = steps[s]
+                if a == 0 and first == 0 and b + LEAD < BLOCKS:
+                    rotate(b + LEAD)
+                e_of[s] = weigh(b, a, first)
+            if 0 <= s - SUM_LAG < len(steps):
+                b, a, first = steps[s - SUM_LAG]
+                add_up(b, a, first, e_of.pop(s - SUM_LAG))
+            if 0 <= s - SUM_LAG - TURN_LAG < len(steps):
+                b, a, first = steps[s - SUM_LAG - TURN_LAG]
+                if first + 2 >= b + 2:
+                    finish(b, a)

@@ -14,10 +14,11 @@ PAIR = H // HK
 SCALE = 0.08838834764831845
 BLOCKS = N // P
 PIECE = 512
+PIECES = N // PIECE
 BLOCKS_IN_PIECE = PIECE // P
 V_STEP = 144
 HUGE = 3.0e38
-LEAD = 1
+LEAD = 2
 SUM_LAG = 3
 TURN_LAG = 2
 
@@ -31,18 +32,17 @@ def tile_openpangusinkattention_b_kernel(tc, table, spread, q, k, v, sink_k, sin
     k_rows = k.rearrange("(a d) n -> d a n", d=P)
     q_halves = q.rearrange("(h s d) n -> s d h n", s=2, d=HALF)
     k_halves = k.rearrange("(a s d) n -> s d a n", s=2, d=HALF)
-    v_blocks = v.rearrange("(b t) (a d) -> b t a d", t=P, a=HK)
+    v_blocks = v.rearrange("(b t) (a d) -> t b a d", t=P, a=HK)
     out_rows = out.rearrange("(h d) n -> d h n", d=P)
 
     with (
         tc.tile_pool(name="held", bufs=1) as held,
-        tc.tile_pool(name="raw", bufs=BLOCKS) as raw,
+        tc.tile_pool(name="raw", bufs=PIECES * HK) as raw,
         tc.tile_pool(name="exps", bufs=SUM_LAG + 2) as exps,
         tc.tile_pool(name="results", bufs=3) as results,
         tc.psum_pool(name="cs_banks", bufs=1) as cs_banks,
-        tc.psum_pool(name="score_banks", bufs=3) as score_banks,
+        tc.psum_pool(name="banks", bufs=4) as banks,
         tc.psum_pool(name="sum_banks", bufs=2) as sum_banks,
-        tc.psum_pool(name="turn_banks", bufs=1) as turn_banks,
     ):
         offsets = held.tile([P, N // 16], U16, name="offsets")
         nc.sync.dma_start(offsets[:], offs)
@@ -59,48 +59,48 @@ def tile_openpangusinkattention_b_kernel(tc, table, spread, q, k, v, sink_k, sin
         nc.gpsimd.memset(v_ones[:, :, :, P:V_STEP], 1.0)
         sink_keys = held.tile([P, HK, P], BF16, name="sink_keys")
 
-        x_of, x_swap_of = [], []
-        for b in range(BLOCKS):
-            cols = slice(b * P, (b + 1) * P)
-            x = raw.tile([P, H + HK, P], F32, name="x")
-            x_swap = raw.tile([P, H + HK, P], F32, name="x_swap")
-            nc.sync.dma_start(x[:, 0:H, :], q_rows[:, :, cols])
-            nc.sync.dma_start(x[:, H:, :], k_rows[:, :, cols])
-            for s in range(2):
-                rows = slice(s * HALF, (s + 1) * HALF)
-                nc.sync.dma_start(x_swap[rows, 0:H, :], q_halves[1 - s, :, :, cols])
-                nc.sync.dma_start(x_swap[rows, H:, :], k_halves[1 - s, :, :, cols])
-            nc.sync.dma_start(v_ones[:, b + 1, :, 0:P], v_blocks[b, :, :, :])
-            x_of.append(x)
-            x_swap_of.append(x_swap)
-            if b == 0:
-                nc.sync.dma_start(sink_keys[:], sink_k.rearrange("(a d) t -> d a t", d=P))
-                nc.sync.dma_start(v_ones[:, 0, :, 0:P], sink_v.rearrange("t (a d) -> t a d", a=HK))
+        x_of, x_swap_of = {}, {}
+        for piece in range(PIECES):
+            cols = slice(piece * PIECE, (piece + 1) * PIECE)
+            for a in range(HK):
+                heads = slice(PAIR * a, PAIR * (a + 1))
+                x = raw.tile([P, PAIR + 1, PIECE], F32, name="x")
+                x_swap = raw.tile([P, PAIR + 1, PIECE], F32, name="x_swap")
+                nc.sync.dma_start(x[:, PAIR, :], k_rows[:, a, cols])
+                nc.sync.dma_start(x[:, 0:PAIR, :], q_rows[:, heads, cols])
+                for s in range(2):
+                    rows = slice(s * HALF, (s + 1) * HALF)
+                    nc.sync.dma_start(x_swap[rows, PAIR, :], k_halves[1 - s, :, a, cols])
+                    nc.sync.dma_start(x_swap[rows, 0:PAIR, :], q_halves[1 - s, :, heads, cols])
+                x_of[piece, a], x_swap_of[piece, a] = x, x_swap
+                if piece == 0:
+                    nc.sync.dma_start(sink_keys[:, a, :], sink_k[a * P : (a + 1) * P, :])
+                    nc.sync.dma_start(v_ones[:, 0, a, 0:P], sink_v[:, a * P : (a + 1) * P])
+                    nc.sync.dma_start(v_ones[:, 1:, a, 0:P], v_blocks[:, :, a, :])
 
         identity_bf16 = held.tile([P, P], BF16, name="identity_bf16")
         make_identity(nc, identity_bf16[:])
         identity_f32 = held.tile([P, P], F32, name="identity_f32")
         make_identity(nc, identity_f32[:])
+        distance = held.tile([P, PAIR, P], I32, name="distance")
+        nc.gpsimd.iota(distance[:], pattern=[[0, PAIR], [1, P]], base=0, channel_multiplier=-1)
+        cap = held.tile([P, PAIR, P], BF16, name="cap")
+        nc.vector.tensor_scalar(cap[:], distance[:], 0.0, HUGE, IS_GE, MULT)
         warm = held.tile([P, 1], F32, name="warm")
         nc.vector.memset(warm[:], 0.0)
         nc.scalar.activation(warm[:], warm[:], EXP)
 
         window = held.tile([P, POSITIONS], BF16, name="window")
         for g in range(4):
-            turned_rows = score_banks.tile([P, 8 * P], BF16, name="turned_rows", tag="scores")
-            for b in range(8):
-                nc.tensor.transpose(turned_rows[:, b * P : (b + 1) * P], table_rows[:, 8 * g + b, :], identity_bf16[:])
+            turned_rows = banks.tile([P, 8 * P], BF16, name="turned_rows", tag="bank")
+            for i in range(8):
+                nc.tensor.transpose(turned_rows[:, i * P : (i + 1) * P], table_rows[:, 8 * g + i, :], identity_bf16[:])
             if g % 2 == 0:
                 nc.vector.tensor_copy(window[:, g * 8 * P : (g + 1) * 8 * P], turned_rows[:])
             else:
                 nc.scalar.copy(window[:, g * 8 * P : (g + 1) * 8 * P], turned_rows[:])
 
-        rotated = held.tile([P, BLOCKS, H + HK, P], BF16, name="rotated")
-
-        distance = held.tile([P, PAIR, P], I32, name="distance")
-        nc.gpsimd.iota(distance[:], pattern=[[0, PAIR], [1, P]], base=0, channel_multiplier=-1)
-        cap = held.tile([P, PAIR, P], BF16, name="cap")
-        nc.vector.tensor_scalar(cap[:], distance[:], 0.0, HUGE, IS_GE, MULT)
+        rotated = held.tile([P, HK, BLOCKS, PAIR + 1, P], BF16, name="rotated")
 
         cs_of, e_of, sums_of, by_query_of = {}, {}, {}, {}
 
@@ -114,69 +114,90 @@ def tile_openpangusinkattention_b_kernel(tc, table, spread, q, k, v, sink_k, sin
                 )
             return cs
 
-        def rotate(b):
+        def rotate(a, b):
             piece = b // BLOCKS_IN_PIECE
-            if b % BLOCKS_IN_PIECE == 0:
+            if piece not in cs_of:
                 cs_of[piece] = look_up(piece)
             cs = cs_of[piece]
             cols = slice((b % BLOCKS_IN_PIECE) * P, (b % BLOCKS_IN_PIECE + 1) * P)
-            x, x_swap = x_of[b], x_swap_of[b]
-            all_heads = [P, H + HK, P]
-            nc.vector.tensor_tensor(x[:], x[:], cs[:, 0, cols].unsqueeze(1).to_broadcast(all_heads), MULT)
-            nc.vector.tensor_tensor(x_swap[:], x_swap[:], cs[:, 1, cols].unsqueeze(1).to_broadcast(all_heads), MULT)
-            nc.gpsimd.tensor_tensor(rotated[:, b, :, :], x[:], x_swap[:], ADD)
+            x, x_swap = x_of[piece, a][:, :, cols], x_swap_of[piece, a][:, :, cols]
+            three = [P, PAIR + 1, P]
+            nc.vector.tensor_tensor(x, x, cs[:, 0, cols].unsqueeze(1).to_broadcast(three), MULT)
+            nc.vector.tensor_tensor(x_swap, x_swap, cs[:, 1, cols].unsqueeze(1).to_broadcast(three), MULT)
+            nc.gpsimd.tensor_tensor(rotated[:, a, b, :, :], x, x_swap, ADD)
 
-        def weigh(b, a, first):
-            key_blocks = range(first, min(first + 2, b + 2))
-            scores = score_banks.tile([P, 2, PAIR, P], F32, name="scores", tag="scores")
-            for i, t in enumerate(key_blocks):
-                keys = sink_keys[:, a, :] if t == 0 else rotated[:, t - 1, H + a, :]
-                nc.tensor.matmul(scores[:, i, :, :], keys, rotated[:, b, PAIR * a : PAIR * (a + 1), :], start=True, stop=True)
-            e = exps.tile([P, 2, PAIR, P], BF16, name="e")
-            count = len(key_blocks)
+        def steps_of(b):
+            return (b + 3) // 2
+
+        def key_blocks(b, step):
+            top = b + 1 - 2 * step
+            return [top, top - 1] if top > 0 else [top]
+
+        def weigh(a, b, step):
+            blocks = key_blocks(b, step)
+            count = len(blocks)
+            scores = banks.tile([P, 2, PAIR, P], F32, name="scores", tag="bank")
+            for i, t in enumerate(blocks):
+                keys = sink_keys[:, a, :] if t == 0 else rotated[:, a, t - 1, PAIR, :]
+                nc.tensor.matmul(scores[:, i, :, :], keys, rotated[:, a, b, 0:PAIR, :], start=True, stop=True)
+            if step == 0:
+                e = exps.tile([P, 2, PAIR, P], BF16, name="e_diagonal")
+            else:
+                e = exps.tile([P, 2, PAIR, P], BF16, name="e")
             nc.scalar.activation(e[:, 0:count, :, :], scores[:, 0:count, :, :], EXP, scale=SCALE)
-            if key_blocks[-1] == b + 1:
-                nc.vector.tensor_tensor(e[:, count - 1, :, :], e[:, count - 1, :, :], cap[:], MIN)
+            if step == 0:
+                nc.vector.tensor_tensor(e[:, 0, :, :], e[:, 0, :, :], cap[:], MIN)
             return e
 
-        def add_up(b, a, first, e):
-            if first == 0:
+        def add_up(a, b, step, e):
+            opening = 1 if steps_of(b) > 1 else 0
+            if step == opening:
                 sums_of[a] = sum_banks.tile([P, PAIR, P + 1], F32, name="sums")
             sums = sums_of[a]
-            for i, t in enumerate(range(first, min(first + 2, b + 2))):
+            blocks = key_blocks(b, step)
+            for i, t in enumerate(blocks):
                 for h in range(PAIR):
                     nc.tensor.matmul(
                         sums[:, h, :], e[:, i, h, :], v_ones[:, t, a, 0 : P + 1],
-                        start=(t == 0 and h == 0), stop=(t == b + 1 and h == PAIR - 1),
+                        start=(step == opening and i == 0 and h == 0),
+                        stop=(step == 0 and i == len(blocks) - 1 and h == PAIR - 1),
                     )
-            if first + 2 >= b + 2:
+            if step == 0:
                 reciprocal = results.tile([P, PAIR, 1], F32, name="reciprocal")
                 nc.vector.reciprocal(reciprocal[:], sums[:, :, P : P + 1])
                 by_query = results.tile([P, PAIR, P], F32, name="by_query")
                 nc.vector.tensor_tensor(by_query[:], sums[:, :, 0:P], reciprocal[:].to_broadcast([P, PAIR, P]), MULT)
-                by_query_of[a] = by_query
+                by_query_of[a, b] = by_query
 
-        def finish(b, a):
-            turned = turn_banks.tile([P, PAIR, P], F32, name="turned")
+        def finish(a, b):
+            by_query = by_query_of.pop((a, b))
+            turned = banks.tile([P, PAIR, P], F32, name="turned", tag="bank")
             for h in range(PAIR):
-                nc.tensor.transpose(turned[:, h, :], by_query_of[a][:, h, :], identity_f32[:])
+                nc.tensor.transpose(turned[:, h, :], by_query[:, h, :], identity_f32[:])
             by_feature = results.tile([P, PAIR, P], F32, name="by_feature")
             nc.vector.tensor_copy(by_feature[:], turned[:])
             nc.sync.dma_start(out_rows[:, PAIR * a : PAIR * (a + 1), b * P : (b + 1) * P], by_feature[:])
 
-        steps = [(b, a, first) for b in range(BLOCKS) for a in range(HK) for first in range(0, b + 2, 2)]
-        for b in range(LEAD):
-            rotate(b)
-        for s in range(len(steps) + SUM_LAG + TURN_LAG):
-            if s < len(steps):
-                b, a, first = steps[s]
-                if a == 0 and first == 0 and b + LEAD < BLOCKS:
-                    rotate(b + LEAD)
-                e_of[s] = weigh(b, a, first)
-            if 0 <= s - SUM_LAG < len(steps):
-                b, a, first = steps[s - SUM_LAG]
-                add_up(b, a, first, e_of.pop(s - SUM_LAG))
-            if 0 <= s - SUM_LAG - TURN_LAG < len(steps):
-                b, a, first = steps[s - SUM_LAG - TURN_LAG]
-                if first + 2 >= b + 2:
-                    finish(b, a)
+        units = [
+            (a, b)
+            for piece in range(PIECES)
+            for a in range(HK)
+            for b in range(piece * BLOCKS_IN_PIECE, (piece + 1) * BLOCKS_IN_PIECE)
+        ]
+        weigh_order = [(u, a, b, step) for u, (a, b) in enumerate(units) for step in range(steps_of(b))]
+        sum_order = [(a, b, step) for a, b in units for step in list(range(1, steps_of(b))) + [0]]
+        for a, b in units[0:LEAD]:
+            rotate(a, b)
+        for i in range(len(weigh_order) + SUM_LAG + TURN_LAG):
+            if i < len(weigh_order):
+                u, a, b, step = weigh_order[i]
+                if step == 0 and u + LEAD < len(units):
+                    rotate(units[u + LEAD][0], units[u + LEAD][1])
+                e_of[a, b, step] = weigh(a, b, step)
+            if 0 <= i - SUM_LAG < len(sum_order):
+                a, b, step = sum_order[i - SUM_LAG]
+                add_up(a, b, step, e_of.pop((a, b, step)))
+            if 0 <= i - SUM_LAG - TURN_LAG < len(sum_order):
+                a, b, step = sum_order[i - SUM_LAG - TURN_LAG]
+                if step == 0:
+                    finish(a, b)

@@ -19,8 +19,8 @@ BLOCKS_IN_PIECE = PIECE // P
 V_STEP = 144
 HUGE = 3.0e38
 LEAD = 2
-SUM_LAG = 3
-TURN_LAG = 2
+SUM_LAG = 5
+TURN_LAG = 5
 
 VISIBLE = P * N + N * (N + 1) // 2
 FLOPS = 2 * P * 2 * P * N + H * VISIBLE * 2 * P * 2
@@ -39,9 +39,8 @@ def tile_openpangusinkattention_b_kernel(tc, table, spread, q, k, v, sink_k, sin
         tc.tile_pool(name="held", bufs=1) as held,
         tc.tile_pool(name="raw", bufs=PIECES * HK) as raw,
         tc.tile_pool(name="exps", bufs=SUM_LAG + 2) as exps,
-        tc.tile_pool(name="results", bufs=3) as results,
-        tc.psum_pool(name="cs_banks", bufs=1) as cs_banks,
-        tc.psum_pool(name="banks", bufs=4) as banks,
+        tc.tile_pool(name="results", bufs=TURN_LAG + 2) as results,
+        tc.psum_pool(name="banks", bufs=6) as banks,
         tc.psum_pool(name="sum_banks", bufs=2) as sum_banks,
     ):
         offsets = held.tile([P, N // 16], U16, name="offsets")
@@ -102,28 +101,30 @@ def tile_openpangusinkattention_b_kernel(tc, table, spread, q, k, v, sink_k, sin
 
         rotated = held.tile([P, HK, BLOCKS, PAIR + 1, P], BF16, name="rotated")
 
-        cs_of, e_of, sums_of, by_query_of = {}, {}, {}, {}
+        e_of, sums_of, by_query_of = {}, {}, {}
 
-        def look_up(piece):
+        cs = held.tile([P, 2, N], F32, name="cs")
+        for piece in range(PIECES):
             piece_offsets = offsets[:, piece * (PIECE // 16) : (piece + 1) * (PIECE // 16)]
-            cs = cs_banks.tile([P, 2, PIECE], F32, name="cs")
             for half in range(2):
+                product = banks.tile([P, PIECE], F32, name="product", tag="bank")
                 nc.tensor.matmul(
-                    cs[:, half, :], spread_sb[:, half * P : (half + 1) * P], window[:].indirect(piece_offsets),
+                    product[:], spread_sb[:, half * P : (half + 1) * P], window[:].indirect(piece_offsets),
                     start=True, stop=True,
                 )
-            return cs
+                if half == 0:
+                    nc.scalar.copy(cs[:, half, piece * PIECE : (piece + 1) * PIECE], product[:])
+                else:
+                    nc.vector.tensor_copy(cs[:, half, piece * PIECE : (piece + 1) * PIECE], product[:])
 
         def rotate(a, b):
             piece = b // BLOCKS_IN_PIECE
-            if piece not in cs_of:
-                cs_of[piece] = look_up(piece)
-            cs = cs_of[piece]
             cols = slice((b % BLOCKS_IN_PIECE) * P, (b % BLOCKS_IN_PIECE + 1) * P)
+            tokens = slice(b * P, (b + 1) * P)
             x, x_swap = x_of[piece, a][:, :, cols], x_swap_of[piece, a][:, :, cols]
             three = [P, PAIR + 1, P]
-            nc.vector.tensor_tensor(x, x, cs[:, 0, cols].unsqueeze(1).to_broadcast(three), MULT)
-            nc.vector.tensor_tensor(x_swap, x_swap, cs[:, 1, cols].unsqueeze(1).to_broadcast(three), MULT)
+            nc.vector.tensor_tensor(x, x, cs[:, 0, tokens].unsqueeze(1).to_broadcast(three), MULT)
+            nc.vector.tensor_tensor(x_swap, x_swap, cs[:, 1, tokens].unsqueeze(1).to_broadcast(three), MULT)
             nc.gpsimd.tensor_tensor(rotated[:, a, b, :, :], x, x_swap, ADD)
 
         def steps_of(b):

@@ -20,7 +20,8 @@ V_STEP = 144
 HUGE = 3.0e38
 LEAD = 2
 SUM_LAG = 5
-TURN_LAG = 5
+SQUARE = 32
+TABLE_GROUPS = 8
 
 VISIBLE = P * N + N * (N + 1) // 2
 FLOPS = 2 * P * 2 * P * N + H * VISIBLE * 2 * P * 2
@@ -33,13 +34,14 @@ def tile_openpangusinkattention_b_kernel(tc, table, spread, q, k, v, sink_k, sin
     q_halves = q.rearrange("(h s d) n -> s d h n", s=2, d=HALF)
     k_halves = k.rearrange("(a s d) n -> s d a n", s=2, d=HALF)
     v_blocks = v.rearrange("(b t) (a d) -> t b a d", t=P, a=HK)
-    out_rows = out.rearrange("(h d) n -> d h n", d=P)
+    out_squares = out.rearrange("(g r) n -> r g n", r=SQUARE)
 
     with (
         tc.tile_pool(name="held", bufs=1) as held,
         tc.tile_pool(name="raw", bufs=PIECES * HK) as raw,
         tc.tile_pool(name="exps", bufs=SUM_LAG + 2) as exps,
-        tc.tile_pool(name="results", bufs=TURN_LAG + 2) as results,
+        tc.tile_pool(name="results", bufs=3) as results,
+        tc.tile_pool(name="stored", bufs=HK * BLOCKS) as stored,
         tc.psum_pool(name="banks", bufs=6) as banks,
         tc.psum_pool(name="sum_banks", bufs=2) as sum_banks,
     ):
@@ -48,9 +50,9 @@ def tile_openpangusinkattention_b_kernel(tc, table, spread, q, k, v, sink_k, sin
 
         table_rows = held.tile([P, POSITIONS // P, P], BF16, name="table_rows")
         table_blocks = table.rearrange("(b p) f -> p b f", p=P)
-        for g in range(4):
+        for g in range(TABLE_GROUPS):
             queue = nc.sync if g % 2 == 0 else nc.scalar
-            queue.dma_start(table_rows[:, 8 * g : 8 * g + 8, :], table_blocks[:, 8 * g : 8 * g + 8, :])
+            queue.dma_start(table_rows[:, 4 * g : 4 * g + 4, :], table_blocks[:, 4 * g : 4 * g + 4, :])
         spread_sb = held.tile([P, 2 * P], BF16, name="spread_sb")
         nc.scalar.dma_start(spread_sb[:], spread)
 
@@ -79,8 +81,6 @@ def tile_openpangusinkattention_b_kernel(tc, table, spread, q, k, v, sink_k, sin
 
         identity_bf16 = held.tile([P, P], BF16, name="identity_bf16")
         make_identity(nc, identity_bf16[:])
-        identity_f32 = held.tile([P, P], F32, name="identity_f32")
-        make_identity(nc, identity_f32[:])
         distance = held.tile([P, PAIR, P], I32, name="distance")
         nc.gpsimd.iota(distance[:], pattern=[[0, PAIR], [1, P]], base=0, channel_multiplier=-1)
         cap = held.tile([P, PAIR, P], BF16, name="cap")
@@ -90,18 +90,18 @@ def tile_openpangusinkattention_b_kernel(tc, table, spread, q, k, v, sink_k, sin
         nc.scalar.activation(warm[:], warm[:], EXP)
 
         window = held.tile([P, POSITIONS], BF16, name="window")
-        for g in range(4):
-            turned_rows = banks.tile([P, 8 * P], BF16, name="turned_rows", tag="bank")
-            for i in range(8):
-                nc.tensor.transpose(turned_rows[:, i * P : (i + 1) * P], table_rows[:, 8 * g + i, :], identity_bf16[:])
+        for g in range(TABLE_GROUPS):
+            turned_rows = banks.tile([P, 4 * P], BF16, name="turned_rows", tag="bank")
+            for i in range(4):
+                nc.tensor.transpose(turned_rows[:, i * P : (i + 1) * P], table_rows[:, 4 * g + i, :], identity_bf16[:])
             if g % 2 == 0:
-                nc.vector.tensor_copy(window[:, g * 8 * P : (g + 1) * 8 * P], turned_rows[:])
+                nc.vector.tensor_copy(window[:, g * 4 * P : (g + 1) * 4 * P], turned_rows[:])
             else:
-                nc.scalar.copy(window[:, g * 8 * P : (g + 1) * 8 * P], turned_rows[:])
+                nc.scalar.copy(window[:, g * 4 * P : (g + 1) * 4 * P], turned_rows[:])
 
         rotated = held.tile([P, HK, BLOCKS, PAIR + 1, P], BF16, name="rotated")
 
-        e_of, sums_of, by_query_of = {}, {}, {}
+        e_of, sums_of = {}, {}
 
         cs = held.tile([P, 2, N], F32, name="cs")
         for piece in range(PIECES):
@@ -166,18 +166,19 @@ def tile_openpangusinkattention_b_kernel(tc, table, spread, q, k, v, sink_k, sin
             if step == 0:
                 reciprocal = results.tile([P, PAIR, 1], F32, name="reciprocal")
                 nc.vector.reciprocal(reciprocal[:], sums[:, :, P : P + 1])
-                by_query = results.tile([P, PAIR, P], F32, name="by_query")
-                nc.vector.tensor_tensor(by_query[:], sums[:, :, 0:P], reciprocal[:].to_broadcast([P, PAIR, P]), MULT)
-                by_query_of[a, b] = by_query
-
-        def finish(a, b):
-            by_query = by_query_of.pop((a, b))
-            turned = banks.tile([P, PAIR, P], F32, name="turned", tag="bank")
-            for h in range(PAIR):
-                nc.tensor.transpose(turned[:, h, :], by_query[:, h, :], identity_f32[:])
-            by_feature = results.tile([P, PAIR, P], F32, name="by_feature")
-            nc.vector.tensor_copy(by_feature[:], turned[:])
-            nc.sync.dma_start(out_rows[:, PAIR * a : PAIR * (a + 1), b * P : (b + 1) * P], by_feature[:])
+                by_query = results.tile([P, PAIR * P], F32, name="by_query", align_bytes=64)
+                nc.vector.tensor_tensor(
+                    by_query[:].rearrange("q (h d) -> q h d", h=PAIR), sums[:, :, 0:P],
+                    reciprocal[:].to_broadcast([P, PAIR, P]), MULT,
+                )
+                squares = stored.tile([P, PAIR * P], F32, name="squares", align_bytes=64)
+                nc.vector.transpose(squares[:], by_query[:])
+                groups = slice(a * PAIR * P // SQUARE, (a + 1) * PAIR * P // SQUARE)
+                for qs in range(P // SQUARE):
+                    nc.sync.dma_start(
+                        out_squares[:, groups, b * P + qs * SQUARE : b * P + (qs + 1) * SQUARE],
+                        squares[qs * SQUARE : (qs + 1) * SQUARE, :].rearrange("r (g c) -> r g c", c=SQUARE),
+                    )
 
         units = [
             (a, b)
@@ -189,7 +190,7 @@ def tile_openpangusinkattention_b_kernel(tc, table, spread, q, k, v, sink_k, sin
         sum_order = [(a, b, step) for a, b in units for step in list(range(1, steps_of(b))) + [0]]
         for a, b in units[0:LEAD]:
             rotate(a, b)
-        for i in range(len(weigh_order) + SUM_LAG + TURN_LAG):
+        for i in range(len(weigh_order) + SUM_LAG):
             if i < len(weigh_order):
                 u, a, b, step = weigh_order[i]
                 if step == 0 and u + LEAD < len(units):
@@ -198,7 +199,3 @@ def tile_openpangusinkattention_b_kernel(tc, table, spread, q, k, v, sink_k, sin
             if 0 <= i - SUM_LAG < len(sum_order):
                 a, b, step = sum_order[i - SUM_LAG]
                 add_up(a, b, step, e_of.pop((a, b, step)))
-            if 0 <= i - SUM_LAG - TURN_LAG < len(sum_order):
-                a, b, step = sum_order[i - SUM_LAG - TURN_LAG]
-                if step == 0:
-                    finish(a, b)

@@ -13,15 +13,16 @@ H, HK = 4, 2
 PAIR = H // HK
 SCALE = 0.08838834764831845
 BLOCKS = N // P
-PIECE = 512
-PIECES = N // PIECE
-BLOCKS_IN_PIECE = PIECE // P
+LOAD = 512
+BLOCKS_IN_LOAD = LOAD // P
+LOOK = 256
+TABLE_GROUP = 8
 V_STEP = 144
-HUGE = 3.0e38
-LEAD = 2
-SUM_LAG = 5
 SQUARE = 32
-TABLE_GROUPS = 8
+HUGE = 3.0e38
+RING = 6
+LEAD = 2
+SUM_LAG = RING - 1
 
 VISIBLE = P * N + N * (N + 1) // 2
 FLOPS = 2 * P * 2 * P * N + H * VISIBLE * 2 * P * 2
@@ -29,30 +30,45 @@ FLOPS = 2 * P * 2 * P * N + H * VISIBLE * 2 * P * 2
 
 def tile_openpangusinkattention_b_kernel(tc, table, spread, q, k, v, sink_k, sink_v, offs, out):
     nc = tc.nc
+    table_blocks = table.rearrange("(b p) f -> p b f", p=P)
     q_rows = q.rearrange("(h d) n -> d h n", d=P)
     k_rows = k.rearrange("(a d) n -> d a n", d=P)
-    q_halves = q.rearrange("(h s d) n -> s d h n", s=2, d=HALF)
-    k_halves = k.rearrange("(a s d) n -> s d a n", s=2, d=HALF)
+    q_halves = q.rearrange("(h side d) n -> side d h n", side=2, d=HALF)
+    k_halves = k.rearrange("(a side d) n -> side d a n", side=2, d=HALF)
     v_blocks = v.rearrange("(b t) (a d) -> t b a d", t=P, a=HK)
-    out_squares = out.rearrange("(g r) n -> r g n", r=SQUARE)
+    out_bands = out.rearrange("(band r) n -> r band n", r=SQUARE)
+
+    units = [
+        (a, b)
+        for load in range(N // LOAD)
+        for a in range(HK)
+        for b in range(load * BLOCKS_IN_LOAD, (load + 1) * BLOCKS_IN_LOAD)
+    ]
+
+    def steps_of(b):
+        return (b + 3) // 2
+
+    def key_blocks(b, step):
+        top = b + 1 - 2 * step
+        return [top, top - 1] if top > 0 else [top]
 
     with (
         tc.tile_pool(name="held", bufs=1) as held,
-        tc.tile_pool(name="raw", bufs=PIECES * HK) as raw,
+        tc.tile_pool(name="raw", bufs=HK * N // LOAD) as raw,
         tc.tile_pool(name="exps", bufs=SUM_LAG + 2) as exps,
         tc.tile_pool(name="results", bufs=3) as results,
-        tc.tile_pool(name="stored", bufs=HK * BLOCKS) as stored,
-        tc.psum_pool(name="banks", bufs=6) as banks,
+        tc.tile_pool(name="stored", bufs=len(units)) as stored,
+        tc.psum_pool(name="ring", bufs=RING) as ring,
         tc.psum_pool(name="sum_banks", bufs=2) as sum_banks,
     ):
         offsets = held.tile([P, N // 16], U16, name="offsets")
         nc.sync.dma_start(offsets[:], offs)
 
         table_rows = held.tile([P, POSITIONS // P, P], BF16, name="table_rows")
-        table_blocks = table.rearrange("(b p) f -> p b f", p=P)
-        for g in range(TABLE_GROUPS):
-            queue = nc.sync if g % 2 == 0 else nc.scalar
-            queue.dma_start(table_rows[:, 4 * g : 4 * g + 4, :], table_blocks[:, 4 * g : 4 * g + 4, :])
+        for group in range(POSITIONS // P // TABLE_GROUP):
+            members = slice(group * TABLE_GROUP, (group + 1) * TABLE_GROUP)
+            queue = nc.sync if group % 2 == 0 else nc.scalar
+            queue.dma_start(table_rows[:, members, :], table_blocks[:, members, :])
         spread_sb = held.tile([P, 2 * P], BF16, name="spread_sb")
         nc.scalar.dma_start(spread_sb[:], spread)
 
@@ -61,26 +77,26 @@ def tile_openpangusinkattention_b_kernel(tc, table, spread, q, k, v, sink_k, sin
         sink_keys = held.tile([P, HK, P], BF16, name="sink_keys")
 
         x_of, x_swap_of = {}, {}
-        for piece in range(PIECES):
-            cols = slice(piece * PIECE, (piece + 1) * PIECE)
+        for load in range(N // LOAD):
+            tokens = slice(load * LOAD, (load + 1) * LOAD)
             for a in range(HK):
                 heads = slice(PAIR * a, PAIR * (a + 1))
-                x = raw.tile([P, PAIR + 1, PIECE], F32, name="x")
-                x_swap = raw.tile([P, PAIR + 1, PIECE], F32, name="x_swap")
-                nc.sync.dma_start(x[:, PAIR, :], k_rows[:, a, cols])
-                nc.sync.dma_start(x[:, 0:PAIR, :], q_rows[:, heads, cols])
-                for s in range(2):
-                    rows = slice(s * HALF, (s + 1) * HALF)
-                    nc.sync.dma_start(x_swap[rows, PAIR, :], k_halves[1 - s, :, a, cols])
-                    nc.sync.dma_start(x_swap[rows, 0:PAIR, :], q_halves[1 - s, :, heads, cols])
-                x_of[piece, a], x_swap_of[piece, a] = x, x_swap
-                if piece == 0:
+                x = raw.tile([P, PAIR + 1, LOAD], F32, name="x")
+                x_swap = raw.tile([P, PAIR + 1, LOAD], F32, name="x_swap")
+                nc.sync.dma_start(x[:, PAIR, :], k_rows[:, a, tokens])
+                nc.sync.dma_start(x[:, 0:PAIR, :], q_rows[:, heads, tokens])
+                for side in range(2):
+                    rows = slice(side * HALF, (side + 1) * HALF)
+                    nc.sync.dma_start(x_swap[rows, PAIR, :], k_halves[1 - side, :, a, tokens])
+                    nc.sync.dma_start(x_swap[rows, 0:PAIR, :], q_halves[1 - side, :, heads, tokens])
+                x_of[load, a], x_swap_of[load, a] = x, x_swap
+                if load == 0:
                     nc.sync.dma_start(sink_keys[:, a, :], sink_k[a * P : (a + 1) * P, :])
                     nc.sync.dma_start(v_ones[:, 0, a, 0:P], sink_v[:, a * P : (a + 1) * P])
                     nc.sync.dma_start(v_ones[:, 1:, a, 0:P], v_blocks[:, :, a, :])
 
-        identity_bf16 = held.tile([P, P], BF16, name="identity_bf16")
-        make_identity(nc, identity_bf16[:])
+        identity = held.tile([P, P], BF16, name="identity")
+        make_identity(nc, identity[:])
         distance = held.tile([P, PAIR, P], I32, name="distance")
         nc.gpsimd.iota(distance[:], pattern=[[0, PAIR], [1, P]], base=0, channel_multiplier=-1)
         cap = held.tile([P, PAIR, P], BF16, name="cap")
@@ -90,62 +106,56 @@ def tile_openpangusinkattention_b_kernel(tc, table, spread, q, k, v, sink_k, sin
         nc.scalar.activation(warm[:], warm[:], EXP)
 
         window = held.tile([P, POSITIONS], BF16, name="window")
-        for g in range(TABLE_GROUPS):
-            turned_rows = banks.tile([P, 4 * P], BF16, name="turned_rows", tag="bank")
-            for i in range(4):
-                nc.tensor.transpose(turned_rows[:, i * P : (i + 1) * P], table_rows[:, 4 * g + i, :], identity_bf16[:])
-            if g % 2 == 0:
-                nc.vector.tensor_copy(window[:, g * 4 * P : (g + 1) * 4 * P], turned_rows[:])
+        for group in range(POSITIONS // P // TABLE_GROUP):
+            turned_rows = ring.tile([P, TABLE_GROUP * P], BF16, name="turned_rows", tag="bank")
+            for member in range(TABLE_GROUP):
+                nc.tensor.transpose(
+                    turned_rows[:, member * P : (member + 1) * P],
+                    table_rows[:, group * TABLE_GROUP + member, :],
+                    identity[:],
+                )
+            positions = slice(group * TABLE_GROUP * P, (group + 1) * TABLE_GROUP * P)
+            if group % 2 == 0:
+                nc.vector.tensor_copy(window[:, positions], turned_rows[:])
             else:
-                nc.scalar.copy(window[:, g * 4 * P : (g + 1) * 4 * P], turned_rows[:])
-
-        rotated = held.tile([P, HK, BLOCKS, PAIR + 1, P], BF16, name="rotated")
-
-        e_of, sums_of = {}, {}
+                nc.scalar.copy(window[:, positions], turned_rows[:])
 
         cs = held.tile([P, 2, N], F32, name="cs")
-        for piece in range(PIECES):
-            piece_offsets = offsets[:, piece * (PIECE // 16) : (piece + 1) * (PIECE // 16)]
+        rotated = held.tile([P, HK, BLOCKS, PAIR + 1, P], BF16, name="rotated")
+        e_of, sums_of = {}, {}
+
+        def look_up(look):
+            tokens = slice(look * LOOK, (look + 1) * LOOK)
+            look_offsets = offsets[:, look * (LOOK // 16) : (look + 1) * (LOOK // 16)]
             for half in range(2):
-                product = banks.tile([P, PIECE], F32, name="product", tag="bank")
+                product = ring.tile([P, LOOK], F32, name="product", tag="bank")
                 nc.tensor.matmul(
-                    product[:], spread_sb[:, half * P : (half + 1) * P], window[:].indirect(piece_offsets),
+                    product[:], spread_sb[:, half * P : (half + 1) * P], window[:].indirect(look_offsets),
                     start=True, stop=True,
                 )
                 if half == 0:
-                    nc.scalar.copy(cs[:, half, piece * PIECE : (piece + 1) * PIECE], product[:])
+                    nc.scalar.copy(cs[:, half, tokens], product[:])
                 else:
-                    nc.vector.tensor_copy(cs[:, half, piece * PIECE : (piece + 1) * PIECE], product[:])
+                    nc.vector.tensor_copy(cs[:, half, tokens], product[:])
 
         def rotate(a, b):
-            piece = b // BLOCKS_IN_PIECE
-            cols = slice((b % BLOCKS_IN_PIECE) * P, (b % BLOCKS_IN_PIECE + 1) * P)
             tokens = slice(b * P, (b + 1) * P)
-            x, x_swap = x_of[piece, a][:, :, cols], x_swap_of[piece, a][:, :, cols]
-            three = [P, PAIR + 1, P]
-            nc.vector.tensor_tensor(x, x, cs[:, 0, tokens].unsqueeze(1).to_broadcast(three), MULT)
-            nc.vector.tensor_tensor(x_swap, x_swap, cs[:, 1, tokens].unsqueeze(1).to_broadcast(three), MULT)
-            nc.gpsimd.tensor_tensor(rotated[:, a, b, :, :], x, x_swap, ADD)
-
-        def steps_of(b):
-            return (b + 3) // 2
-
-        def key_blocks(b, step):
-            top = b + 1 - 2 * step
-            return [top, top - 1] if top > 0 else [top]
+            cols = slice((b % BLOCKS_IN_LOAD) * P, (b % BLOCKS_IN_LOAD + 1) * P)
+            x_b = x_of[b // BLOCKS_IN_LOAD, a][:, :, cols]
+            x_swap_b = x_swap_of[b // BLOCKS_IN_LOAD, a][:, :, cols]
+            three_heads = [P, PAIR + 1, P]
+            nc.vector.tensor_tensor(x_b, x_b, cs[:, 0, tokens].unsqueeze(1).to_broadcast(three_heads), MULT)
+            nc.vector.tensor_tensor(x_swap_b, x_swap_b, cs[:, 1, tokens].unsqueeze(1).to_broadcast(three_heads), MULT)
+            nc.gpsimd.tensor_tensor(rotated[:, a, b, :, :], x_b, x_swap_b, ADD)
 
         def weigh(a, b, step):
             blocks = key_blocks(b, step)
-            count = len(blocks)
-            scores = banks.tile([P, 2, PAIR, P], F32, name="scores", tag="bank")
-            for i, t in enumerate(blocks):
+            scores = ring.tile([P, 2, PAIR, P], F32, name="scores", tag="bank")
+            for slot, t in enumerate(blocks):
                 keys = sink_keys[:, a, :] if t == 0 else rotated[:, a, t - 1, PAIR, :]
-                nc.tensor.matmul(scores[:, i, :, :], keys, rotated[:, a, b, 0:PAIR, :], start=True, stop=True)
-            if step == 0:
-                e = exps.tile([P, 2, PAIR, P], BF16, name="e_diagonal")
-            else:
-                e = exps.tile([P, 2, PAIR, P], BF16, name="e")
-            nc.scalar.activation(e[:, 0:count, :, :], scores[:, 0:count, :, :], EXP, scale=SCALE)
+                nc.tensor.matmul(scores[:, slot, :, :], keys, rotated[:, a, b, 0:PAIR, :], start=True, stop=True)
+            e = exps.tile([P, 2, PAIR, P], BF16, name="e", tag="e_diagonal" if step == 0 else "e")
+            nc.scalar.activation(e[:, 0 : len(blocks), :, :], scores[:, 0 : len(blocks), :, :], EXP, scale=SCALE)
             if step == 0:
                 nc.vector.tensor_tensor(e[:, 0, :, :], e[:, 0, :, :], cap[:], MIN)
             return e
@@ -156,46 +166,44 @@ def tile_openpangusinkattention_b_kernel(tc, table, spread, q, k, v, sink_k, sin
                 sums_of[a] = sum_banks.tile([P, PAIR, P + 1], F32, name="sums")
             sums = sums_of[a]
             blocks = key_blocks(b, step)
-            for i, t in enumerate(blocks):
+            for slot, t in enumerate(blocks):
                 for h in range(PAIR):
                     nc.tensor.matmul(
-                        sums[:, h, :], e[:, i, h, :], v_ones[:, t, a, 0 : P + 1],
-                        start=(step == opening and i == 0 and h == 0),
-                        stop=(step == 0 and i == len(blocks) - 1 and h == PAIR - 1),
+                        sums[:, h, :], e[:, slot, h, :], v_ones[:, t, a, 0 : P + 1],
+                        start=(step == opening and slot == 0 and h == 0),
+                        stop=(step == 0 and slot == len(blocks) - 1 and h == PAIR - 1),
                     )
-            if step == 0:
-                reciprocal = results.tile([P, PAIR, 1], F32, name="reciprocal")
-                nc.vector.reciprocal(reciprocal[:], sums[:, :, P : P + 1])
-                by_query = results.tile([P, PAIR * P], F32, name="by_query", align_bytes=64)
-                nc.vector.tensor_tensor(
-                    by_query[:].rearrange("q (h d) -> q h d", h=PAIR), sums[:, :, 0:P],
-                    reciprocal[:].to_broadcast([P, PAIR, P]), MULT,
+            if step > 0:
+                return
+            reciprocal = results.tile([P, PAIR, 1], F32, name="reciprocal")
+            nc.vector.reciprocal(reciprocal[:], sums[:, :, P : P + 1])
+            by_query = results.tile([P, PAIR * P], F32, name="by_query", align_bytes=64)
+            nc.vector.tensor_tensor(
+                by_query[:].rearrange("q (h d) -> q h d", h=PAIR), sums[:, :, 0:P],
+                reciprocal[:].to_broadcast([P, PAIR, P]), MULT,
+            )
+            squares = stored.tile([P, PAIR * P], F32, name="squares", align_bytes=64)
+            nc.vector.transpose(squares[:], by_query[:])
+            bands = slice(a * PAIR * P // SQUARE, (a + 1) * PAIR * P // SQUARE)
+            for i in range(P // SQUARE):
+                nc.sync.dma_start(
+                    out_bands[:, bands, b * P + i * SQUARE : b * P + (i + 1) * SQUARE],
+                    squares[i * SQUARE : (i + 1) * SQUARE, :].rearrange("r (band c) -> r band c", c=SQUARE),
                 )
-                squares = stored.tile([P, PAIR * P], F32, name="squares", align_bytes=64)
-                nc.vector.transpose(squares[:], by_query[:])
-                groups = slice(a * PAIR * P // SQUARE, (a + 1) * PAIR * P // SQUARE)
-                for qs in range(P // SQUARE):
-                    nc.sync.dma_start(
-                        out_squares[:, groups, b * P + qs * SQUARE : b * P + (qs + 1) * SQUARE],
-                        squares[qs * SQUARE : (qs + 1) * SQUARE, :].rearrange("r (g c) -> r g c", c=SQUARE),
-                    )
 
-        units = [
-            (a, b)
-            for piece in range(PIECES)
-            for a in range(HK)
-            for b in range(piece * BLOCKS_IN_PIECE, (piece + 1) * BLOCKS_IN_PIECE)
-        ]
-        weigh_order = [(u, a, b, step) for u, (a, b) in enumerate(units) for step in range(steps_of(b))]
-        sum_order = [(a, b, step) for a, b in units for step in list(range(1, steps_of(b))) + [0]]
+        look_up(0)
         for a, b in units[0:LEAD]:
             rotate(a, b)
-        for i in range(len(weigh_order) + SUM_LAG):
-            if i < len(weigh_order):
-                u, a, b, step = weigh_order[i]
+        for look in range(1, N // LOOK):
+            look_up(look)
+        weigh_order = [(u, a, b, step) for u, (a, b) in enumerate(units) for step in range(steps_of(b))]
+        sum_order = [(a, b, step) for a, b in units for step in list(range(1, steps_of(b))) + [0]]
+        for now in range(len(weigh_order) + SUM_LAG):
+            if now < len(weigh_order):
+                u, a, b, step = weigh_order[now]
                 if step == 0 and u + LEAD < len(units):
                     rotate(units[u + LEAD][0], units[u + LEAD][1])
                 e_of[a, b, step] = weigh(a, b, step)
-            if 0 <= i - SUM_LAG < len(sum_order):
-                a, b, step = sum_order[i - SUM_LAG]
+            if now >= SUM_LAG:
+                a, b, step = sum_order[now - SUM_LAG]
                 add_up(a, b, step, e_of.pop((a, b, step)))

@@ -15,8 +15,8 @@ SCALE = 0.08838834764831845
 BLOCKS = N // P
 LOAD = 512
 BLOCKS_IN_LOAD = LOAD // P
-LOOK = 256
-TABLE_GROUP = 8
+LOOK = 512
+TABLE_GROUP = 4
 V_STEP = 144
 SQUARE = 32
 HUGE = 3.0e38

@@ -146,7 +146,7 @@ def tile_openpangusinkattention_b_kernel(tc, table, spread, q, k, v, sink_k, sin
             three_heads = [P, PAIR + 1, P]
             nc.vector.tensor_tensor(x_b, x_b, cs[:, 0, tokens].unsqueeze(1).to_broadcast(three_heads), MULT)
             nc.vector.tensor_tensor(x_swap_b, x_swap_b, cs[:, 1, tokens].unsqueeze(1).to_broadcast(three_heads), MULT)
-            nc.gpsimd.tensor_tensor(rotated[:, a, b, :, :], x_b, x_swap_b, ADD)
+            nc.vector.tensor_tensor(rotated[:, a, b, :, :], x_b, x_swap_b, ADD)
 
         def weigh(a, b, step):
             blocks = key_blocks(b, step)

@@ -15,13 +15,17 @@ SCALE = 0.08838834764831845
 BLOCKS = N // P
 LOAD = 512
 BLOCKS_IN_LOAD = LOAD // P
-LOOK = 512
+LOADS = N // LOAD
+LOOK = 256
+LOOKS = N // LOOK
 TABLE_GROUP = 4
+TABLE_GROUPS = POSITIONS // P // TABLE_GROUP
 V_STEP = 144
 SQUARE = 32
 HUGE = 3.0e38
 RING = 6
-LEAD = 2
+STEPS_PER_ROTATION = 3
+FIRST_SPREAD_STEP = 6
 SUM_LAG = RING - 1
 
 VISIBLE = P * N + N * (N + 1) // 2
@@ -30,7 +34,7 @@ FLOPS = 2 * P * 2 * P * N + H * VISIBLE * 2 * P * 2
 
 def tile_openpangusinkattention_b_kernel(tc, table, spread, q, k, v, sink_k, sink_v, offs, out):
     nc = tc.nc
-    table_blocks = table.rearrange("(b p) f -> p b f", p=P)
+    table_groups = table.rearrange("(group p member) f -> p group member f", p=P, member=TABLE_GROUP)
     q_rows = q.rearrange("(h d) n -> d h n", d=P)
     k_rows = k.rearrange("(a d) n -> d a n", d=P)
     q_halves = q.rearrange("(h side d) n -> side d h n", side=2, d=HALF)
@@ -38,12 +42,7 @@ def tile_openpangusinkattention_b_kernel(tc, table, spread, q, k, v, sink_k, sin
     v_blocks = v.rearrange("(b t) (a d) -> t b a d", t=P, a=HK)
     out_bands = out.rearrange("(band r) n -> r band n", r=SQUARE)
 
-    units = [
-        (a, b)
-        for load in range(N // LOAD)
-        for a in range(HK)
-        for b in range(load * BLOCKS_IN_LOAD, (load + 1) * BLOCKS_IN_LOAD)
-    ]
+    units = [(a, b) for a in range(HK) for b in reversed(range(BLOCKS))]
 
     def steps_of(b):
         return (b + 3) // 2
@@ -54,7 +53,7 @@ def tile_openpangusinkattention_b_kernel(tc, table, spread, q, k, v, sink_k, sin
 
     with (
         tc.tile_pool(name="held", bufs=1) as held,
-        tc.tile_pool(name="raw", bufs=HK * N // LOAD) as raw,
+        tc.tile_pool(name="raw", bufs=HK * LOADS) as raw,
         tc.tile_pool(name="exps", bufs=SUM_LAG + 2) as exps,
         tc.tile_pool(name="results", bufs=3) as results,
         tc.tile_pool(name="stored", bufs=len(units)) as stored,
@@ -64,11 +63,10 @@ def tile_openpangusinkattention_b_kernel(tc, table, spread, q, k, v, sink_k, sin
         offsets = held.tile([P, N // 16], U16, name="offsets")
         nc.sync.dma_start(offsets[:], offs)
 
-        table_rows = held.tile([P, POSITIONS // P, P], BF16, name="table_rows")
-        for group in range(POSITIONS // P // TABLE_GROUP):
-            members = slice(group * TABLE_GROUP, (group + 1) * TABLE_GROUP)
+        table_rows = held.tile([P, TABLE_GROUPS, TABLE_GROUP, P], BF16, name="table_rows")
+        for group in range(TABLE_GROUPS):
             queue = nc.sync if group % 2 == 0 else nc.scalar
-            queue.dma_start(table_rows[:, members, :], table_blocks[:, members, :])
+            queue.dma_start(table_rows[:, group, :, :], table_groups[:, group, :, :])
         spread_sb = held.tile([P, 2 * P], BF16, name="spread_sb")
         nc.scalar.dma_start(spread_sb[:], spread)
 
@@ -77,23 +75,27 @@ def tile_openpangusinkattention_b_kernel(tc, table, spread, q, k, v, sink_k, sin
         sink_keys = held.tile([P, HK, P], BF16, name="sink_keys")
 
         x_of, x_swap_of = {}, {}
-        for load in range(N // LOAD):
+
+        def load_heads(kind, a, load):
             tokens = slice(load * LOAD, (load + 1) * LOAD)
-            for a in range(HK):
-                heads = slice(PAIR * a, PAIR * (a + 1))
-                x = raw.tile([P, PAIR + 1, LOAD], F32, name="x")
-                x_swap = raw.tile([P, PAIR + 1, LOAD], F32, name="x_swap")
-                nc.sync.dma_start(x[:, PAIR, :], k_rows[:, a, tokens])
-                nc.sync.dma_start(x[:, 0:PAIR, :], q_rows[:, heads, tokens])
-                for side in range(2):
-                    rows = slice(side * HALF, (side + 1) * HALF)
-                    nc.sync.dma_start(x_swap[rows, PAIR, :], k_halves[1 - side, :, a, tokens])
-                    nc.sync.dma_start(x_swap[rows, 0:PAIR, :], q_halves[1 - side, :, heads, tokens])
-                x_of[load, a], x_swap_of[load, a] = x, x_swap
-                if load == 0:
-                    nc.sync.dma_start(sink_keys[:, a, :], sink_k[a * P : (a + 1) * P, :])
-                    nc.sync.dma_start(v_ones[:, 0, a, 0:P], sink_v[:, a * P : (a + 1) * P])
-                    nc.sync.dma_start(v_ones[:, 1:, a, 0:P], v_blocks[:, :, a, :])
+            heads = slice(a, a + 1) if kind == "k" else slice(PAIR * a, PAIR * (a + 1))
+            rows, halves = (k_rows, k_halves) if kind == "k" else (q_rows, q_halves)
+            x = raw.tile([P, heads.stop - heads.start, LOAD], F32, name="x", tag="x_" + kind)
+            x_swap = raw.tile([P, heads.stop - heads.start, LOAD], F32, name="x_swap", tag="x_swap_" + kind)
+            nc.sync.dma_start(x[:], rows[:, heads, tokens])
+            for side in range(2):
+                nc.sync.dma_start(x_swap[side * HALF : (side + 1) * HALF, :, :], halves[1 - side, :, heads, tokens])
+            x_of[kind, a, load], x_swap_of[kind, a, load] = x, x_swap
+
+        for a in range(HK):
+            load_heads("q", a, LOADS - 1)
+            nc.sync.dma_start(sink_keys[:, a, :], sink_k[a * P : (a + 1) * P, :])
+            for load in range(LOADS):
+                load_heads("k", a, load)
+            nc.sync.dma_start(v_ones[:, 0, a, 0:P], sink_v[:, a * P : (a + 1) * P])
+            nc.sync.dma_start(v_ones[:, 1:, a, 0:P], v_blocks[:, :, a, :])
+            for load in reversed(range(LOADS - 1)):
+                load_heads("q", a, load)
 
         identity = held.tile([P, P], BF16, name="identity")
         make_identity(nc, identity[:])
@@ -106,74 +108,74 @@ def tile_openpangusinkattention_b_kernel(tc, table, spread, q, k, v, sink_k, sin
         nc.scalar.activation(warm[:], warm[:], EXP)
 
         window = held.tile([P, POSITIONS], BF16, name="window")
-        for group in range(POSITIONS // P // TABLE_GROUP):
-            turned_rows = ring.tile([P, TABLE_GROUP * P], BF16, name="turned_rows", tag="bank")
+        for group in range(TABLE_GROUPS):
+            turned_rows = ring.tile([P, TABLE_GROUP, P], BF16, name="turned_rows", tag="bank")
             for member in range(TABLE_GROUP):
-                nc.tensor.transpose(
-                    turned_rows[:, member * P : (member + 1) * P],
-                    table_rows[:, group * TABLE_GROUP + member, :],
-                    identity[:],
-                )
-            positions = slice(group * TABLE_GROUP * P, (group + 1) * TABLE_GROUP * P)
+                nc.tensor.transpose(turned_rows[:, member, :], table_rows[:, group, member, :], identity[:])
+            in_order = turned_rows[:].rearrange("f member p -> f p member")
+            columns = window[:, group * TABLE_GROUP * P : (group + 1) * TABLE_GROUP * P]
+            columns = columns.rearrange("f (p member) -> f p member", member=TABLE_GROUP)
             if group % 2 == 0:
-                nc.vector.tensor_copy(window[:, positions], turned_rows[:])
+                nc.vector.tensor_copy(columns, in_order)
             else:
-                nc.scalar.copy(window[:, positions], turned_rows[:])
+                nc.scalar.copy(columns, in_order)
 
         cs = held.tile([P, 2, N], F32, name="cs")
-        rotated = held.tile([P, HK, BLOCKS, PAIR + 1, P], BF16, name="rotated")
+        rotated_q = held.tile([P, HK, BLOCKS, PAIR, P], BF16, name="rotated_q")
+        rotated_k = held.tile([P, HK, 1, N], BF16, name="rotated_k")
         e_of, sums_of = {}, {}
 
         def look_up(look):
             tokens = slice(look * LOOK, (look + 1) * LOOK)
             look_offsets = offsets[:, look * (LOOK // 16) : (look + 1) * (LOOK // 16)]
+            product = ring.tile([P, 2, LOOK], F32, name="product", tag="bank")
             for half in range(2):
-                product = ring.tile([P, LOOK], F32, name="product", tag="bank")
                 nc.tensor.matmul(
-                    product[:], spread_sb[:, half * P : (half + 1) * P], window[:].indirect(look_offsets),
+                    product[:, half, :], spread_sb[:, half * P : (half + 1) * P], window[:].indirect(look_offsets),
                     start=True, stop=True,
                 )
-                if half == 0:
-                    nc.scalar.copy(cs[:, half, tokens], product[:])
-                else:
-                    nc.vector.tensor_copy(cs[:, half, tokens], product[:])
+            nc.scalar.copy(cs[:, :, tokens], product[:])
 
-        def rotate(a, b):
-            tokens = slice(b * P, (b + 1) * P)
-            cols = slice((b % BLOCKS_IN_LOAD) * P, (b % BLOCKS_IN_LOAD + 1) * P)
-            x_b = x_of[b // BLOCKS_IN_LOAD, a][:, :, cols]
-            x_swap_b = x_swap_of[b // BLOCKS_IN_LOAD, a][:, :, cols]
-            three_heads = [P, PAIR + 1, P]
-            nc.vector.tensor_tensor(x_b, x_b, cs[:, 0, tokens].unsqueeze(1).to_broadcast(three_heads), MULT)
-            nc.vector.tensor_tensor(x_swap_b, x_swap_b, cs[:, 1, tokens].unsqueeze(1).to_broadcast(three_heads), MULT)
-            nc.vector.tensor_tensor(rotated[:, a, b, :, :], x_b, x_swap_b, ADD)
+        def rotate(result, kind, a, first_block, blocks):
+            tokens = slice(first_block * P, (first_block + blocks) * P)
+            cols = slice((first_block % BLOCKS_IN_LOAD) * P, (first_block % BLOCKS_IN_LOAD + blocks) * P)
+            x = x_of[kind, a, first_block // BLOCKS_IN_LOAD][:, :, cols]
+            x_swap = x_swap_of[kind, a, first_block // BLOCKS_IN_LOAD][:, :, cols]
+            nc.vector.tensor_tensor(x, x, cs[:, 0, tokens].unsqueeze(1).to_broadcast(list(x.shape)), MULT)
+            nc.vector.tensor_tensor(x_swap, x_swap, cs[:, 1, tokens].unsqueeze(1).to_broadcast(list(x.shape)), MULT)
+            nc.vector.tensor_tensor(result, x, x_swap, ADD)
+
+        def rotate_queries(a, b):
+            rotate(rotated_q[:, a, b, :, :], "q", a, b, 1)
+
+        def rotate_keys(a, first_block, blocks):
+            rotate(rotated_k[:, a, :, first_block * P : (first_block + blocks) * P], "k", a, first_block, blocks)
 
         def weigh(a, b, step):
             blocks = key_blocks(b, step)
             scores = ring.tile([P, 2, PAIR, P], F32, name="scores", tag="bank")
             for slot, t in enumerate(blocks):
-                keys = sink_keys[:, a, :] if t == 0 else rotated[:, a, t - 1, PAIR, :]
-                nc.tensor.matmul(scores[:, slot, :, :], keys, rotated[:, a, b, 0:PAIR, :], start=True, stop=True)
+                keys = sink_keys[:, a, :] if t == 0 else rotated_k[:, a, 0, (t - 1) * P : t * P]
+                nc.tensor.matmul(scores[:, slot, :, :], keys, rotated_q[:, a, b, :, :], start=True, stop=True)
             e = exps.tile([P, 2, PAIR, P], BF16, name="e", tag="e_diagonal" if step == 0 else "e")
             nc.scalar.activation(e[:, 0 : len(blocks), :, :], scores[:, 0 : len(blocks), :, :], EXP, scale=SCALE)
             if step == 0:
                 nc.vector.tensor_tensor(e[:, 0, :, :], e[:, 0, :, :], cap[:], MIN)
             return e
 
-        def add_up(a, b, step, e):
-            opening = 1 if steps_of(b) > 1 else 0
-            if step == opening:
-                sums_of[a] = sum_banks.tile([P, PAIR, P + 1], F32, name="sums")
-            sums = sums_of[a]
+        def add_up(a, b, step, e, opening, closing):
+            if opening:
+                sums_of[a, b] = sum_banks.tile([P, PAIR, P + 1], F32, name="sums")
+            sums = sums_of[a, b]
             blocks = key_blocks(b, step)
             for slot, t in enumerate(blocks):
                 for h in range(PAIR):
                     nc.tensor.matmul(
                         sums[:, h, :], e[:, slot, h, :], v_ones[:, t, a, 0 : P + 1],
-                        start=(step == opening and slot == 0 and h == 0),
-                        stop=(step == 0 and slot == len(blocks) - 1 and h == PAIR - 1),
+                        start=(opening and slot == 0 and h == 0),
+                        stop=(closing and slot == len(blocks) - 1 and h == PAIR - 1),
                     )
-            if step > 0:
+            if not closing:
                 return
             reciprocal = results.tile([P, PAIR, 1], F32, name="reciprocal")
             nc.vector.reciprocal(reciprocal[:], sums[:, :, P : P + 1])
@@ -191,19 +193,41 @@ def tile_openpangusinkattention_b_kernel(tc, table, spread, q, k, v, sink_k, sin
                     squares[i * SQUARE : (i + 1) * SQUARE, :].rearrange("r (band c) -> r band c", c=SQUARE),
                 )
 
-        look_up(0)
-        for a, b in units[0:LEAD]:
-            rotate(a, b)
-        for look in range(1, N // LOOK):
+        (a, b), (a_beside, b_beside) = units[0:2]
+        side_by_side = []
+        for step in reversed(range(steps_of(b))):
+            side_by_side.append((a, b, step))
+            if step > 0:
+                side_by_side.append((a_beside, b_beside, step - 1))
+        weigh_order = side_by_side + [(a, b, step) for a, b in units[2:] for step in range(steps_of(b))]
+        sum_order = side_by_side + [(a, b, step) for a, b in units[2:] for step in list(range(1, steps_of(b))) + [0]]
+        opening_steps = {(a, b): step for a, b, step in reversed(sum_order)}
+        closing_steps = {(a, b): step for a, b, step in sum_order}
+
+        at_once = [
+            (rotate_queries, (0, BLOCKS - 1)),
+            (rotate_queries, (0, BLOCKS - 2)),
+            (rotate_keys, (0, 0, BLOCKS_IN_LOAD // 2)),
+            (rotate_keys, (0, BLOCKS_IN_LOAD // 2, BLOCKS_IN_LOAD // 2)),
+        ]
+        at_once.extend((rotate_keys, (0, load * BLOCKS_IN_LOAD, BLOCKS_IN_LOAD)) for load in range(1, LOADS))
+        spread_out = [(rotate_queries, (0, b)) for b in reversed(range(BLOCKS - 2))]
+        spread_out.append((rotate_queries, (1, BLOCKS - 1)))
+        spread_out.extend((rotate_keys, (1, load * BLOCKS_IN_LOAD, BLOCKS_IN_LOAD)) for load in reversed(range(LOADS)))
+        spread_out.extend((rotate_queries, (1, b)) for b in reversed(range(BLOCKS - 1)))
+
+        for look in [LOOKS - 1] + list(range(LOOKS - 1)):
             look_up(look)
-        weigh_order = [(u, a, b, step) for u, (a, b) in enumerate(units) for step in range(steps_of(b))]
-        sum_order = [(a, b, step) for a, b in units for step in list(range(1, steps_of(b))) + [0]]
+        for rotation, what in at_once:
+            rotation(*what)
         for now in range(len(weigh_order) + SUM_LAG):
             if now < len(weigh_order):
-                u, a, b, step = weigh_order[now]
-                if step == 0 and u + LEAD < len(units):
-                    rotate(units[u + LEAD][0], units[u + LEAD][1])
+                a, b, step = weigh_order[now]
+                turn = now - FIRST_SPREAD_STEP
+                if turn >= 0 and turn % STEPS_PER_ROTATION == 0 and turn // STEPS_PER_ROTATION < len(spread_out):
+                    rotation, what = spread_out[turn // STEPS_PER_ROTATION]
+                    rotation(*what)
                 e_of[a, b, step] = weigh(a, b, step)
             if now >= SUM_LAG:
                 a, b, step = sum_order[now - SUM_LAG]
-                add_up(a, b, step, e_of.pop((a, b, step)))
+                add_up(a, b, step, e_of.pop((a, b, step)), step == opening_steps[a, b], step == closing_steps[a, b])

@@ -42,7 +42,11 @@ def tile_openpangusinkattention_b_kernel(tc, table, spread, q, k, v, sink_k, sin
     v_blocks = v.rearrange("(b t) (a d) -> t b a d", t=P, a=HK)
     out_bands = out.rearrange("(band r) n -> r band n", r=SQUARE)
 
-    units = [(a, b) for a in range(HK) for b in reversed(range(BLOCKS))]
+    def large_and_small(blocks):
+        return [blocks[-1 - i // 2] if i % 2 == 0 else blocks[i // 2] for i in range(len(blocks))]
+
+    block_order = [BLOCKS - 1] + large_and_small(list(range(BLOCKS - 1)))
+    units = [(a, b) for a in range(HK) for b in block_order]
 
     def steps_of(b):
         return (b + 3) // 2
@@ -74,18 +78,17 @@ def tile_openpangusinkattention_b_kernel(tc, table, spread, q, k, v, sink_k, sin
         nc.gpsimd.memset(v_ones[:, :, :, P:V_STEP], 1.0)
         sink_keys = held.tile([P, HK, P], BF16, name="sink_keys")
 
-        x_of, x_swap_of = {}, {}
+        x_of = {}
 
         def load_heads(kind, a, load):
             tokens = slice(load * LOAD, (load + 1) * LOAD)
             heads = slice(a, a + 1) if kind == "k" else slice(PAIR * a, PAIR * (a + 1))
             rows, halves = (k_rows, k_halves) if kind == "k" else (q_rows, q_halves)
-            x = raw.tile([P, heads.stop - heads.start, LOAD], F32, name="x", tag="x_" + kind)
-            x_swap = raw.tile([P, heads.stop - heads.start, LOAD], F32, name="x_swap", tag="x_swap_" + kind)
-            nc.sync.dma_start(x[:], rows[:, heads, tokens])
+            x = raw.tile([P, 2, heads.stop - heads.start, LOAD], F32, name="x", tag="x_" + kind)
+            nc.sync.dma_start(x[:, 0, :, :], rows[:, heads, tokens])
             for side in range(2):
-                nc.sync.dma_start(x_swap[side * HALF : (side + 1) * HALF, :, :], halves[1 - side, :, heads, tokens])
-            x_of[kind, a, load], x_swap_of[kind, a, load] = x, x_swap
+                nc.sync.dma_start(x[side * HALF : (side + 1) * HALF, 1, :, :], halves[1 - side, :, heads, tokens])
+            x_of[kind, a, load] = x
 
         for a in range(HK):
             load_heads("q", a, LOADS - 1)
@@ -94,7 +97,7 @@ def tile_openpangusinkattention_b_kernel(tc, table, spread, q, k, v, sink_k, sin
                 load_heads("k", a, load)
             nc.sync.dma_start(v_ones[:, 0, a, 0:P], sink_v[:, a * P : (a + 1) * P])
             nc.sync.dma_start(v_ones[:, 1:, a, 0:P], v_blocks[:, :, a, :])
-            for load in reversed(range(LOADS - 1)):
+            for load in range(LOADS - 1):
                 load_heads("q", a, load)
 
         identity = held.tile([P, P], BF16, name="identity")
@@ -139,11 +142,9 @@ def tile_openpangusinkattention_b_kernel(tc, table, spread, q, k, v, sink_k, sin
         def rotate(result, kind, a, first_block, blocks):
             tokens = slice(first_block * P, (first_block + blocks) * P)
             cols = slice((first_block % BLOCKS_IN_LOAD) * P, (first_block % BLOCKS_IN_LOAD + blocks) * P)
-            x = x_of[kind, a, first_block // BLOCKS_IN_LOAD][:, :, cols]
-            x_swap = x_swap_of[kind, a, first_block // BLOCKS_IN_LOAD][:, :, cols]
-            nc.vector.tensor_tensor(x, x, cs[:, 0, tokens].unsqueeze(1).to_broadcast(list(x.shape)), MULT)
-            nc.vector.tensor_tensor(x_swap, x_swap, cs[:, 1, tokens].unsqueeze(1).to_broadcast(list(x.shape)), MULT)
-            nc.vector.tensor_tensor(result, x, x_swap, ADD)
+            x = x_of[kind, a, first_block // BLOCKS_IN_LOAD][:, :, :, cols]
+            nc.vector.tensor_tensor(x, x, cs[:, :, tokens].unsqueeze(2).to_broadcast(list(x.shape)), MULT)
+            nc.vector.tensor_tensor(result, x[:, 0, :, :], x[:, 1, :, :], ADD)
 
         def rotate_queries(a, b):
             rotate(rotated_q[:, a, b, :, :], "q", a, b, 1)
@@ -157,7 +158,7 @@ def tile_openpangusinkattention_b_kernel(tc, table, spread, q, k, v, sink_k, sin
             for slot, t in enumerate(blocks):
                 keys = sink_keys[:, a, :] if t == 0 else rotated_k[:, a, 0, (t - 1) * P : t * P]
                 nc.tensor.matmul(scores[:, slot, :, :], keys, rotated_q[:, a, b, :, :], start=True, stop=True)
-            e = exps.tile([P, 2, PAIR, P], BF16, name="e", tag="e_diagonal" if step == 0 else "e")
+            e = exps.tile([P, 2, PAIR, P], BF16, name="e")
             nc.scalar.activation(e[:, 0 : len(blocks), :, :], scores[:, 0 : len(blocks), :, :], EXP, scale=SCALE)
             if step == 0:
                 nc.vector.tensor_tensor(e[:, 0, :, :], e[:, 0, :, :], cap[:], MIN)
@@ -194,40 +195,33 @@ def tile_openpangusinkattention_b_kernel(tc, table, spread, q, k, v, sink_k, sin
                 )
 
         (a, b), (a_beside, b_beside) = units[0:2]
-        side_by_side = []
-        for step in reversed(range(steps_of(b))):
-            side_by_side.append((a, b, step))
-            if step > 0:
-                side_by_side.append((a_beside, b_beside, step - 1))
-        weigh_order = side_by_side + [(a, b, step) for a, b in units[2:] for step in range(steps_of(b))]
-        sum_order = side_by_side + [(a, b, step) for a, b in units[2:] for step in list(range(1, steps_of(b))) + [0]]
-        opening_steps = {(a, b): step for a, b, step in reversed(sum_order)}
-        closing_steps = {(a, b): step for a, b, step in sum_order}
+        assert steps_of(b) == steps_of(b_beside) + 1 and len(key_blocks(b, steps_of(b) - 1)) == 1
+        side_by_side = [(a, b, steps_of(b) - 1)]
+        for step in reversed(range(steps_of(b_beside))):
+            side_by_side.extend([(a, b, step), (a_beside, b_beside, step)])
+        order = side_by_side + [(a, b, step) for a, b in units[2:] for step in range(steps_of(b))]
+        opening_steps = {(a, b): step for a, b, step in reversed(order)}
+        closing_steps = {(a, b): step for a, b, step in order}
 
-        at_once = [
-            (rotate_queries, (0, BLOCKS - 1)),
-            (rotate_queries, (0, BLOCKS - 2)),
-            (rotate_keys, (0, 0, BLOCKS_IN_LOAD // 2)),
-            (rotate_keys, (0, BLOCKS_IN_LOAD // 2, BLOCKS_IN_LOAD // 2)),
-        ]
-        at_once.extend((rotate_keys, (0, load * BLOCKS_IN_LOAD, BLOCKS_IN_LOAD)) for load in range(1, LOADS))
-        spread_out = [(rotate_queries, (0, b)) for b in reversed(range(BLOCKS - 2))]
-        spread_out.append((rotate_queries, (1, BLOCKS - 1)))
+        at_once = [(rotate_queries, (0, BLOCKS - 1)), (rotate_keys, (0, 0, 2)), (rotate_queries, (0, BLOCKS - 2))]
+        at_once.extend((rotate_keys, (0, first_block, 2)) for first_block in range(2, BLOCKS, 2))
+        spread_out = [(rotate_queries, (0, b)) for b in block_order[2:]]
+        spread_out.append((rotate_queries, (1, block_order[0])))
         spread_out.extend((rotate_keys, (1, load * BLOCKS_IN_LOAD, BLOCKS_IN_LOAD)) for load in reversed(range(LOADS)))
-        spread_out.extend((rotate_queries, (1, b)) for b in reversed(range(BLOCKS - 1)))
+        spread_out.extend((rotate_queries, (1, b)) for b in block_order[1:])
 
         for look in [LOOKS - 1] + list(range(LOOKS - 1)):
             look_up(look)
         for rotation, what in at_once:
             rotation(*what)
-        for now in range(len(weigh_order) + SUM_LAG):
-            if now < len(weigh_order):
-                a, b, step = weigh_order[now]
+        for now in range(len(order) + SUM_LAG):
+            if now < len(order):
+                a, b, step = order[now]
                 turn = now - FIRST_SPREAD_STEP
                 if turn >= 0 and turn % STEPS_PER_ROTATION == 0 and turn // STEPS_PER_ROTATION < len(spread_out):
                     rotation, what = spread_out[turn // STEPS_PER_ROTATION]
                     rotation(*what)
                 e_of[a, b, step] = weigh(a, b, step)
             if now >= SUM_LAG:
-                a, b, step = sum_order[now - SUM_LAG]
+                a, b, step = order[now - SUM_LAG]
                 add_up(a, b, step, e_of.pop((a, b, step)), step == opening_steps[a, b], step == closing_steps[a, b])

@@ -64,15 +64,14 @@ def tile_openpangusinkattention_b_kernel(tc, table, spread, q, k, v, sink_k, sin
         tc.psum_pool(name="ring", bufs=RING) as ring,
         tc.psum_pool(name="sum_banks", bufs=2) as sum_banks,
     ):
-        offsets = held.tile([P, N // 16], U16, name="offsets")
-        nc.sync.dma_start(offsets[:], offs)
-
         table_rows = held.tile([P, TABLE_GROUPS, TABLE_GROUP, P], BF16, name="table_rows")
         for group in range(TABLE_GROUPS):
             queue = nc.sync if group % 2 == 0 else nc.scalar
             queue.dma_start(table_rows[:, group, :, :], table_groups[:, group, :, :])
         spread_sb = held.tile([P, 2 * P], BF16, name="spread_sb")
-        nc.scalar.dma_start(spread_sb[:], spread)
+        nc.sync.dma_start(spread_sb[:], spread)
+        offsets = held.tile([P, N // 16], U16, name="offsets")
+        nc.sync.dma_start(offsets[:], offs)
 
         v_ones = held.tile([P, BLOCKS + 1, HK, V_STEP], BF16, name="v_ones")
         nc.gpsimd.memset(v_ones[:, :, :, P:V_STEP], 1.0)
@@ -91,24 +90,25 @@ def tile_openpangusinkattention_b_kernel(tc, table, spread, q, k, v, sink_k, sin
             x_of[kind, a, load] = x
 
         for a in range(HK):
+            load_heads("k", a, 0)
             load_heads("q", a, LOADS - 1)
             nc.sync.dma_start(sink_keys[:, a, :], sink_k[a * P : (a + 1) * P, :])
-            for load in range(LOADS):
+            for load in range(1, LOADS):
                 load_heads("k", a, load)
             nc.sync.dma_start(v_ones[:, 0, a, 0:P], sink_v[:, a * P : (a + 1) * P])
             nc.sync.dma_start(v_ones[:, 1:, a, 0:P], v_blocks[:, :, a, :])
             for load in range(LOADS - 1):
                 load_heads("q", a, load)
 
+        warm = held.tile([P, 1], F32, name="warm")
+        nc.vector.memset(warm[:], 0.0)
+        nc.scalar.activation(warm[:], warm[:], EXP)
         identity = held.tile([P, P], BF16, name="identity")
         make_identity(nc, identity[:])
         distance = held.tile([P, PAIR, P], I32, name="distance")
         nc.gpsimd.iota(distance[:], pattern=[[0, PAIR], [1, P]], base=0, channel_multiplier=-1)
         cap = held.tile([P, PAIR, P], BF16, name="cap")
         nc.vector.tensor_scalar(cap[:], distance[:], 0.0, HUGE, IS_GE, MULT)
-        warm = held.tile([P, 1], F32, name="warm")
-        nc.vector.memset(warm[:], 0.0)
-        nc.scalar.activation(warm[:], warm[:], EXP)
 
         window = held.tile([P, POSITIONS], BF16, name="window")
         for group in range(TABLE_GROUPS):
@@ -203,14 +203,14 @@ def tile_openpangusinkattention_b_kernel(tc, table, spread, q, k, v, sink_k, sin
         opening_steps = {(a, b): step for a, b, step in reversed(order)}
         closing_steps = {(a, b): step for a, b, step in order}
 
-        at_once = [(rotate_queries, (0, BLOCKS - 1)), (rotate_keys, (0, 0, 2)), (rotate_queries, (0, BLOCKS - 2))]
+        at_once = [(rotate_keys, (0, 0, 2)), (rotate_queries, (0, BLOCKS - 1)), (rotate_queries, (0, BLOCKS - 2))]
         at_once.extend((rotate_keys, (0, first_block, 2)) for first_block in range(2, BLOCKS, 2))
         spread_out = [(rotate_queries, (0, b)) for b in block_order[2:]]
         spread_out.append((rotate_queries, (1, block_order[0])))
         spread_out.extend((rotate_keys, (1, load * BLOCKS_IN_LOAD, BLOCKS_IN_LOAD)) for load in reversed(range(LOADS)))
         spread_out.extend((rotate_queries, (1, b)) for b in block_order[1:])
 
-        for look in [LOOKS - 1] + list(range(LOOKS - 1)):
+        for look in [0, LOOKS - 1] + list(range(1, LOOKS - 1)):
             look_up(look)
         for rotation, what in at_once:
             rotation(*what)

@@ -20,6 +20,7 @@ LOOK = 256
 LOOKS = N // LOOK
 TABLE_GROUP = 4
 TABLE_GROUPS = POSITIONS // P // TABLE_GROUP
+SUM_STEP = 256
 V_STEP = 144
 SQUARE = 32
 HUGE = 3.0e38
@@ -166,8 +167,8 @@ def tile_openpangusinkattention_b_kernel(tc, table, spread, q, k, v, sink_k, sin
 
         def add_up(a, b, step, e, opening, closing):
             if opening:
-                sums_of[a, b] = sum_banks.tile([P, PAIR, P + 1], F32, name="sums")
-            sums = sums_of[a, b]
+                sums_of[a, b] = sum_banks.tile([P, PAIR, SUM_STEP], F32, name="sums")
+            sums = sums_of[a, b][:, :, 0 : P + 1]
             blocks = key_blocks(b, step)
             for slot, t in enumerate(blocks):
                 for h in range(PAIR):

import concourse.mybir as mybir
from concourse.masks import make_identity

BF16, F32, I32, U16 = mybir.dt.bfloat16, mybir.dt.float32, mybir.dt.int32, mybir.dt.uint16
MULT, ADD, MIN, IS_GE = mybir.AluOpType.mult, mybir.AluOpType.add, mybir.AluOpType.min, mybir.AluOpType.is_ge
EXP = mybir.ActivationFunctionType.Exp

P = 128
HALF = 64
POSITIONS = 4096
N = 1536
H, HK = 4, 2
PAIR = H // HK
SCALE = 0.08838834764831845
BLOCKS = N // P
LOAD = 512
BLOCKS_IN_LOAD = LOAD // P
LOADS = N // LOAD
LOOK = 256
LOOKS = N // LOOK
TABLE_GROUP = 4
TABLE_GROUPS = POSITIONS // P // TABLE_GROUP
SUM_STEP = 256
V_STEP = 144
SQUARE = 32
HUGE = 3.0e38
RING = 6
STEPS_PER_ROTATION = 3
FIRST_SPREAD_STEP = 6
SUM_LAG = RING - 1

VISIBLE = P * N + N * (N + 1) // 2
FLOPS = 2 * P * 2 * P * N + H * VISIBLE * 2 * P * 2


def tile_openpangusinkattention_b_kernel(tc, table, spread, q, k, v, sink_k, sink_v, offs, out):
    nc = tc.nc
    table_groups = table.rearrange("(group p member) f -> p group member f", p=P, member=TABLE_GROUP)
    q_rows = q.rearrange("(h d) n -> d h n", d=P)
    k_rows = k.rearrange("(a d) n -> d a n", d=P)
    q_halves = q.rearrange("(h side d) n -> side d h n", side=2, d=HALF)
    k_halves = k.rearrange("(a side d) n -> side d a n", side=2, d=HALF)
    v_blocks = v.rearrange("(b t) (a d) -> t b a d", t=P, a=HK)
    out_bands = out.rearrange("(band r) n -> r band n", r=SQUARE)

    def large_and_small(blocks):
        return [blocks[-1 - i // 2] if i % 2 == 0 else blocks[i // 2] for i in range(len(blocks))]

    block_order = [BLOCKS - 1] + large_and_small(list(range(BLOCKS - 1)))
    units = [(a, b) for a in range(HK) for b in block_order]

    def steps_of(b):
        return (b + 3) // 2

    def key_blocks(b, step):
        top = b + 1 - 2 * step
        return [top, top - 1] if top > 0 else [top]

    with (
        tc.tile_pool(name="held", bufs=1) as held,
        tc.tile_pool(name="raw", bufs=HK * LOADS) as raw,
        tc.tile_pool(name="exps", bufs=SUM_LAG + 2) as exps,
        tc.tile_pool(name="results", bufs=3) as results,
        tc.tile_pool(name="stored", bufs=len(units)) as stored,
        tc.psum_pool(name="ring", bufs=RING) as ring,
        tc.psum_pool(name="sum_banks", bufs=2) as sum_banks,
    ):
        table_rows = held.tile([P, TABLE_GROUPS, TABLE_GROUP, P], BF16, name="table_rows")
        for group in range(TABLE_GROUPS):
            queue = nc.sync if group % 2 == 0 else nc.scalar
            queue.dma_start(table_rows[:, group, :, :], table_groups[:, group, :, :])
        spread_sb = held.tile([P, 2 * P], BF16, name="spread_sb")
        nc.sync.dma_start(spread_sb[:], spread)
        offsets = held.tile([P, N // 16], U16, name="offsets")
        nc.sync.dma_start(offsets[:], offs)

        v_ones = held.tile([P, BLOCKS + 1, HK, V_STEP], BF16, name="v_ones")
        nc.gpsimd.memset(v_ones[:, :, :, P:V_STEP], 1.0)
        sink_keys = held.tile([P, HK, P], BF16, name="sink_keys")

        x_of = {}

        def load_heads(kind, a, load):
            tokens = slice(load * LOAD, (load + 1) * LOAD)
            heads = slice(a, a + 1) if kind == "k" else slice(PAIR * a, PAIR * (a + 1))
            rows, halves = (k_rows, k_halves) if kind == "k" else (q_rows, q_halves)
            x = raw.tile([P, 2, heads.stop - heads.start, LOAD], F32, name="x", tag="x_" + kind)
            nc.sync.dma_start(x[:, 0, :, :], rows[:, heads, tokens])
            for side in range(2):
                nc.sync.dma_start(x[side * HALF : (side + 1) * HALF, 1, :, :], halves[1 - side, :, heads, tokens])
            x_of[kind, a, load] = x

        for a in range(HK):
            load_heads("k", a, 0)
            load_heads("q", a, LOADS - 1)
            nc.sync.dma_start(sink_keys[:, a, :], sink_k[a * P : (a + 1) * P, :])
            for load in range(1, LOADS):
                load_heads("k", a, load)
            nc.sync.dma_start(v_ones[:, 0, a, 0:P], sink_v[:, a * P : (a + 1) * P])
            nc.sync.dma_start(v_ones[:, 1:, a, 0:P], v_blocks[:, :, a, :])
            for load in range(LOADS - 1):
                load_heads("q", a, load)

        warm = held.tile([P, 1], F32, name="warm")
        nc.vector.memset(warm[:], 0.0)
        nc.scalar.activation(warm[:], warm[:], EXP)
        identity = held.tile([P, P], BF16, name="identity")
        make_identity(nc, identity[:])
        distance = held.tile([P, PAIR, P], I32, name="distance")
        nc.gpsimd.iota(distance[:], pattern=[[0, PAIR], [1, P]], base=0, channel_multiplier=-1)
        cap = held.tile([P, PAIR, P], BF16, name="cap")
        nc.vector.tensor_scalar(cap[:], distance[:], 0.0, HUGE, IS_GE, MULT)

        window = held.tile([P, POSITIONS], BF16, name="window")
        for group in range(TABLE_GROUPS):
            turned_rows = ring.tile([P, TABLE_GROUP, P], BF16, name="turned_rows", tag="bank")
            for member in range(TABLE_GROUP):
                nc.tensor.transpose(turned_rows[:, member, :], table_rows[:, group, member, :], identity[:])
            in_order = turned_rows[:].rearrange("f member p -> f p member")
            columns = window[:, group * TABLE_GROUP * P : (group + 1) * TABLE_GROUP * P]
            columns = columns.rearrange("f (p member) -> f p member", member=TABLE_GROUP)
            if group % 2 == 0:
                nc.vector.tensor_copy(columns, in_order)
            else:
                nc.scalar.copy(columns, in_order)

        cs = held.tile([P, 2, N], F32, name="cs")
        rotated_q = held.tile([P, HK, BLOCKS, PAIR, P], BF16, name="rotated_q")
        rotated_k = held.tile([P, HK, 1, N], BF16, name="rotated_k")
        e_of, sums_of = {}, {}

        def look_up(look):
            tokens = slice(look * LOOK, (look + 1) * LOOK)
            look_offsets = offsets[:, look * (LOOK // 16) : (look + 1) * (LOOK // 16)]
            product = ring.tile([P, 2, LOOK], F32, name="product", tag="bank")
            for half in range(2):
                nc.tensor.matmul(
                    product[:, half, :], spread_sb[:, half * P : (half + 1) * P], window[:].indirect(look_offsets),
                    start=True, stop=True,
                )
            nc.scalar.copy(cs[:, :, tokens], product[:])

        def rotate(result, kind, a, first_block, blocks):
            tokens = slice(first_block * P, (first_block + blocks) * P)
            cols = slice((first_block % BLOCKS_IN_LOAD) * P, (first_block % BLOCKS_IN_LOAD + blocks) * P)
            x = x_of[kind, a, first_block // BLOCKS_IN_LOAD][:, :, :, cols]
            nc.vector.tensor_tensor(x, x, cs[:, :, tokens].unsqueeze(2).to_broadcast(list(x.shape)), MULT)
            nc.vector.tensor_tensor(result, x[:, 0, :, :], x[:, 1, :, :], ADD)

        def rotate_queries(a, b):
            rotate(rotated_q[:, a, b, :, :], "q", a, b, 1)

        def rotate_keys(a, first_block, blocks):
            rotate(rotated_k[:, a, :, first_block * P : (first_block + blocks) * P], "k", a, first_block, blocks)

        def weigh(a, b, step):
            blocks = key_blocks(b, step)
            scores = ring.tile([P, 2, PAIR, P], F32, name="scores", tag="bank")
            for slot, t in enumerate(blocks):
                keys = sink_keys[:, a, :] if t == 0 else rotated_k[:, a, 0, (t - 1) * P : t * P]
                nc.tensor.matmul(scores[:, slot, :, :], keys, rotated_q[:, a, b, :, :], start=True, stop=True)
            e = exps.tile([P, 2, PAIR, P], BF16, name="e")
            nc.scalar.activation(e[:, 0 : len(blocks), :, :], scores[:, 0 : len(blocks), :, :], EXP, scale=SCALE)
            if step == 0:
                nc.vector.tensor_tensor(e[:, 0, :, :], e[:, 0, :, :], cap[:], MIN)
            return e

        def add_up(a, b, step, e, opening, closing):
            if opening:
                sums_of[a, b] = sum_banks.tile([P, PAIR, SUM_STEP], F32, name="sums")
            sums = sums_of[a, b][:, :, 0 : P + 1]
            blocks = key_blocks(b, step)
            for slot, t in enumerate(blocks):
                for h in range(PAIR):
                    nc.tensor.matmul(
                        sums[:, h, :], e[:, slot, h, :], v_ones[:, t, a, 0 : P + 1],
                        start=(opening and slot == 0 and h == 0),
                        stop=(closing and slot == len(blocks) - 1 and h == PAIR - 1),
                    )
            if not closing:
                return
            reciprocal = results.tile([P, PAIR, 1], F32, name="reciprocal")
            nc.vector.reciprocal(reciprocal[:], sums[:, :, P : P + 1])
            by_query = results.tile([P, PAIR * P], F32, name="by_query", align_bytes=64)
            nc.vector.tensor_tensor(
                by_query[:].rearrange("q (h d) -> q h d", h=PAIR), sums[:, :, 0:P],
                reciprocal[:].to_broadcast([P, PAIR, P]), MULT,
            )
            squares = stored.tile([P, PAIR * P], F32, name="squares", align_bytes=64)
            nc.vector.transpose(squares[:], by_query[:])
            bands = slice(a * PAIR * P // SQUARE, (a + 1) * PAIR * P // SQUARE)
            for i in range(P // SQUARE):
                nc.sync.dma_start(
                    out_bands[:, bands, b * P + i * SQUARE : b * P + (i + 1) * SQUARE],
                    squares[i * SQUARE : (i + 1) * SQUARE, :].rearrange("r (band c) -> r band c", c=SQUARE),
                )

        (a, b), (a_beside, b_beside) = units[0:2]
        assert steps_of(b) == steps_of(b_beside) + 1 and len(key_blocks(b, steps_of(b) - 1)) == 1
        side_by_side = [(a, b, steps_of(b) - 1)]
        for step in reversed(range(steps_of(b_beside))):
            side_by_side.extend([(a, b, step), (a_beside, b_beside, step)])
        order = side_by_side + [(a, b, step) for a, b in units[2:] for step in range(steps_of(b))]
        opening_steps = {(a, b): step for a, b, step in reversed(order)}
        closing_steps = {(a, b): step for a, b, step in order}

        at_once = [(rotate_keys, (0, 0, 2)), (rotate_queries, (0, BLOCKS - 1)), (rotate_queries, (0, BLOCKS - 2))]
        at_once.extend((rotate_keys, (0, first_block, 2)) for first_block in range(2, BLOCKS, 2))
        spread_out = [(rotate_queries, (0, b)) for b in block_order[2:]]
        spread_out.append((rotate_queries, (1, block_order[0])))
        spread_out.extend((rotate_keys, (1, load * BLOCKS_IN_LOAD, BLOCKS_IN_LOAD)) for load in reversed(range(LOADS)))
        spread_out.extend((rotate_queries, (1, b)) for b in block_order[1:])

        for look in [0, LOOKS - 1] + list(range(1, LOOKS - 1)):
            look_up(look)
        for rotation, what in at_once:
            rotation(*what)
        for now in range(len(order) + SUM_LAG):
            if now < len(order):
                a, b, step = order[now]
                turn = now - FIRST_SPREAD_STEP
                if turn >= 0 and turn % STEPS_PER_ROTATION == 0 and turn // STEPS_PER_ROTATION < len(spread_out):
                    rotation, what = spread_out[turn // STEPS_PER_ROTATION]
                    rotation(*what)
                e_of[a, b, step] = weigh(a, b, step)
            if now >= SUM_LAG:
                a, b, step = order[now - SUM_LAG]
                add_up(a, b, step, e_of.pop((a, b, step)), step == opening_steps[a, b], step == closing_steps[a, b])
